import numpy as np
import ml_dtypes


def mxq(x, axis, fmt="e4m3"):
    dtype, down = {"e4m3": (ml_dtypes.float8_e4m3fn, 7), "e5m2": (ml_dtypes.float8_e5m2, 14)}[fmt]
    v = np.moveaxis(np.asarray(x, np.float32).astype(ml_dtypes.bfloat16).astype(np.float64), axis, -1)
    blocks = v.reshape(v.shape[:-1] + (-1, 32))
    amax = np.abs(blocks).max(-1, keepdims=True)
    byte = np.maximum(np.where(amax > 0, np.frexp(amax)[1] - 1 + 127, 0) - down, 1)
    scale = np.exp2(byte - 127.0)
    codes = (blocks / scale).astype(np.float32).astype(dtype).astype(np.float64)
    return np.moveaxis((codes * scale).reshape(v.shape), -1, axis)


WIDE = False


def mx_kscale(k):
    if not WIDE:
        return np.ones(k)
    levels = np.array([10, -10, 5, -5, 0])
    a = np.random.permutation(np.resize(levels, k // 512 * 4)).reshape(k // 512, 4)
    idx = np.arange(k)
    return np.exp2(a[idx // 512, idx % 128 // 32])


BF16 = ml_dtypes.bfloat16


def bf(x):
    return np.asarray(x, np.float32).astype(BF16)


def f64(x):
    return np.asarray(x).astype(np.float64)


E2M1 = np.array([0.0, 0.5, 1.0, 1.5, 2.0, 3.0, 4.0, 6.0, -0.0, -0.5, -1.0, -1.5, -2.0, -3.0, -4.0, -6.0])


def pack_weight(w, fmt):
    k, n = w.shape
    w = f64(bf(w)).reshape(k // 32, 32, n)
    amax = np.abs(w).max(1)
    if fmt == "e4m3":
        byte = np.frexp(amax)[1] - 1 + 127 - 7
    else:
        mant, ex = np.frexp(amax / 6.0)
        byte = np.where(mant > 0.5, ex, ex - 1) + 127
    byte = np.clip(np.where(amax > 0, byte, 1), 1, 254)
    scaled = (w * np.exp2(127.0 - byte)[:, None, :]).reshape(k, n).astype(np.float32)
    by_word = np.ascontiguousarray(scaled.reshape(k // 512, 128, 4, n).transpose(0, 1, 3, 2))
    if fmt == "e4m3":
        words = by_word.astype(ml_dtypes.float8_e4m3fn).view(np.uint8)
    else:
        c = by_word.astype(ml_dtypes.float4_e2m1fn).view(np.uint8) & 0xF
        words = c[..., 0::2] | (c[..., 1::2] << 4)
    return np.ascontiguousarray(words), np.ascontiguousarray(byte.astype(np.uint8).reshape(k // 512, 16, n))


def unpack_weight(words, scales, fmt):
    g, p, n, _ = words.shape
    if fmt == "e4m3":
        vals = np.ascontiguousarray(words).view(ml_dtypes.float8_e4m3fn).astype(np.float64)
    else:
        nib = np.empty((g, p, n, 4), np.uint8)
        nib[..., 0::2] = words & 0xF
        nib[..., 1::2] = words >> 4
        vals = E2M1[nib]
    vals = vals * np.repeat(np.exp2(scales.astype(np.float64) - 127.0), 8, axis=1)[..., None]
    return vals.transpose(0, 1, 3, 2).reshape(g * 512, n)


B, IN_DIM, MEM = 8192, 256, 256
DIN = MEM + IN_DIM
MIN_TS, MAX_TS, EPS = 0.1, 10.0, 1e-6


def sigmoid(v):
    return 1.0 / (1.0 + np.exp(-v))


def setup_inputs():
    s = mx_kscale(DIN)[MEM:]
    r = np.concatenate([np.ones(MEM), s])
    x = bf(np.random.standard_normal((B, IN_DIM)) * s)
    h = bf(np.random.standard_normal((B, MEM)))
    h_candidate = bf(np.tanh(0.7 * np.random.standard_normal((B, MEM))))
    Wd_words, Wd_scales = pack_weight(np.random.standard_normal((DIN, MEM)) * 1.3 / np.sqrt(DIN) / r[:, None], "e4m3")
    bd = bf(np.random.standard_normal(MEM) * 0.5)
    Wu_words, Wu_scales = pack_weight(np.random.standard_normal((DIN, MEM)) * 1.3 / np.sqrt(DIN) / r[:, None], "e4m3")
    bu = bf(np.random.standard_normal(MEM) * 0.5)
    return {"x": x,
            "h": h,
            "h_candidate": h_candidate,
            "Wd_words": Wd_words,
            "Wd_scales": Wd_scales,
            "bd": bd,
            "Wu_words": Wu_words,
            "Wu_scales": Wu_scales,
            "bu": bu}


def reference(x, h, h_candidate, Wd_words, Wd_scales, bd, Wu_words, Wu_scales, bu):
    h = f64(h)
    cq = mxq(np.concatenate([h, f64(x)], axis=-1), 1, "e4m3")
    decay = sigmoid((cq @ unpack_weight(Wd_words, Wd_scales, "e4m3")) + f64(bd))
    update = sigmoid((cq @ unpack_weight(Wu_words, Wu_scales, "e4m3")) + f64(bu))
    decay = MIN_TS + (MAX_TS - MIN_TS) * decay + EPS
    new_h = (1.0 - update) * (h / decay) + update * f64(h_candidate)
    h_norm = np.maximum(np.sqrt(np.square(h).sum(-1, keepdims=True)), EPS)
    nh_norm = np.maximum(np.sqrt(np.square(new_h).sum(-1, keepdims=True)), 1e-12)
    return new_h / nh_norm * h_norm

@@ -1,0 +1,271 @@
+import math
+from contextlib import ExitStack
+
+import concourse.mybir as mybir
+from concourse.masks import make_identity
+
+F32 = mybir.dt.float32
+BF16 = mybir.dt.bfloat16
+I32 = mybir.dt.int32
+U32 = mybir.dt.uint32
+U8 = mybir.dt.uint8
+FP8X4 = mybir.dt.float8_e4m3fn_x4
+ACT = mybir.ActivationFunctionType
+ALU = mybir.AluOpType
+
+P = 128
+ROWS = 8192
+FEAT = 256
+K = 2 * FEAT
+TILES = 4
+GROUP_ROWS = TILES * P
+GROUPS = ROWS // GROUP_ROWS
+PAIRS = TILES // 2
+BLOCKS = 4
+LOAD_AHEAD = 4
+FIRST_STEP = -2
+LAST_STEP = GROUPS + 1
+
+FLOPS = 2 * ROWS * K * 2 * FEAT
+
+LEAST_DECAY = 0.1 + 1e-6
+SPAN = 10.0 - 0.1
+MOST_DECAY = LEAST_DECAY + SPAN
+SHIFT = math.log(MOST_DECAY / LEAST_DECAY)
+BETA = SPAN / (LEAST_DECAY * MOST_DECAY)
+KEEP_FLOOR = LEAST_DECAY / SPAN
+H_SQ_FLOOR = 1e-6 * 1e-6
+M_SQ_FLOOR = (1e-12 / BETA) * (1e-12 / BETA)
+
+
+def live(g):
+    return 0 <= g < GROUPS
+
+
+def tile_liquidmemorycell_pb_t_kernel(
+    tc, x, h, h_candidate, Wd_words, Wd_scales, bd, Wu_words, Wu_scales, bu, out
+):
+    nc = tc.nc
+    h_rows = h.rearrange("(g p j) f -> g p j f", p=P, j=TILES)
+    x_rows = x.rearrange("(g p j) f -> g p j f", p=P, j=TILES)
+    cand_rows = h_candidate.rearrange("(g p j) f -> g p j f", p=P, j=TILES)
+    out_rows = out.rearrange("(g p j) f -> g p j f", p=P, j=TILES)
+
+    with ExitStack() as stack:
+        const = stack.enter_context(tc.tile_pool(name="const", bufs=1))
+        rows_in = stack.enter_context(tc.tile_pool(name="rows_in", bufs=LOAD_AHEAD + 2))
+        quant = stack.enter_context(tc.tile_pool(name="quant", bufs=2))
+        gates_sb = stack.enter_context(tc.tile_pool(name="gates_sb", bufs=2))
+        work = stack.enter_context(tc.tile_pool(name="work", bufs=PAIRS))
+        rows_out = stack.enter_context(tc.tile_pool(name="rows_out", bufs=3))
+        stats = stack.enter_context(tc.tile_pool(name="stats", bufs=6))
+        ct_ps = stack.enter_context(tc.psum_pool(name="ct_ps", bufs=2))
+        sum_ps = stack.enter_context(tc.psum_pool(name="sum_ps", bufs=2))
+        back_ps = stack.enter_context(tc.psum_pool(name="back_ps", bufs=PAIRS))
+        stack.enter_context(tc.manual_schedule())
+
+        c_tiles, cand_tiles, code_tiles, plane_tiles = {}, {}, {}, {}
+        gate_tiles, keep_banks, update_banks = {}, {}, {}
+        m_tiles, h_sq_tiles, factor_tiles = {}, {}, {}
+
+        def load(g):
+            c_tile = rows_in.tile([P, TILES, K], BF16)
+            nc.sync.dma_start(out=c_tile[:, :, 0:FEAT], in_=h_rows[g])
+            nc.sync.dma_start(out=c_tile[:, :, FEAT:K], in_=x_rows[g])
+            cand = rows_in.tile([P, TILES, FEAT], BF16)
+            nc.sync.dma_start(out=cand[:], in_=cand_rows[g])
+            c_tiles[g] = c_tile
+            cand_tiles[g] = cand
+
+        def h_square_sums(g):
+            h_sq = stats.tile([P, TILES], F32)
+            unread = work.tile([P, TILES, FEAT], BF16, name="unread_h")
+            for j in range(TILES):
+                nc.scalar.activation(
+                    out=unread[:, j, :], in_=c_tiles[g][:, j, 0:FEAT], func=ACT.Square, accum_out=h_sq[:, j : j + 1]
+                )
+            h_sq_tiles[g] = h_sq
+
+        def quantise_c(g):
+            c_words = c_tiles[g][:].rearrange("p j k -> p (j k)").bitcast(F32)
+            words_in_row = K // 2
+            grouped = quant.tile([P, GROUP_ROWS * 4], BF16, align_bytes=64)
+            grouped_words = grouped[:].bitcast(F32).rearrange("p (j b u) -> p j b u", j=TILES, u=2)
+            for pair in range(PAIRS):
+                planes = ct_ps.tile([P, 2, 2, P], F32)
+                for jj in range(2):
+                    first = (2 * pair + jj) * words_in_row
+                    for u in range(2):
+                        nc.tensor.transpose(
+                            planes[:, jj, u, :], c_words[:, first + u : first + words_in_row : 2], identity[:]
+                        )
+                nc.scalar.copy(
+                    out=grouped_words[:, 2 * pair : 2 * pair + 2], in_=planes[:].rearrange("p j u b -> p j b u")
+                )
+            codes = quant.tile([P, GROUP_ROWS], U32, align_bytes=64)
+            plane = quant.tile([P, GROUP_ROWS], U8, align_bytes=64)
+            nc.vector.quantize_mx(out=codes[:].bitcast(FP8X4), scales=plane[:], in_=grouped[:])
+            code_tiles[g] = codes
+            plane_tiles[g] = plane
+
+        def gates(g, blocks):
+            if g not in gate_tiles:
+                gate_T = gates_sb.tile([P, BLOCKS, GROUP_ROWS], F32)
+                gate_tiles[g] = gate_T
+            sums = {}
+            for blk in blocks:
+                acc = sum_ps.tile([P, GROUP_ROWS], F32)
+                cols = slice(blk * P, (blk + 1) * P)
+                nc.tensor.matmul_mx(
+                    out=acc[:],
+                    lhsT=w_words[:, cols].bitcast(FP8X4),
+                    lhsT_scale=w_plane[:, cols],
+                    rhs=code_tiles[g][:].bitcast(FP8X4),
+                    rhs_scale=plane_tiles[g][:],
+                    start=True,
+                    stop=True,
+                )
+                sums[blk] = acc
+            for blk in blocks:
+                nc.scalar.activation(
+                    out=gate_tiles[g][:, blk, :],
+                    in_=sums[blk][:],
+                    func=ACT.Sigmoid,
+                    bias=bias_cols[:, blk : blk + 1],
+                    scale=(-1.0 if blk < 2 else 1.0),
+                )
+
+        def bring_back(g):
+            for first_blk, banks, label in ((0, keep_banks, "keep_ps"), (2, update_banks, "update_ps")):
+                for pair in range(PAIRS):
+                    bank = back_ps.tile([P, 2, FEAT], F32, name=label)
+                    for jj in range(2):
+                        rows = slice((2 * pair + jj) * P, (2 * pair + jj + 1) * P)
+                        for half in range(2):
+                            nc.tensor.transpose(
+                                bank[:, jj, half * P : (half + 1) * P],
+                                gate_tiles[g][:, first_blk + half, rows],
+                                identity[:],
+                            )
+                    banks[g, pair] = bank
+
+        def blend(g):
+            m_tile = rows_out.tile([P, TILES, FEAT], F32)
+            old, gap, step = {}, {}, {}
+            for pair in range(PAIRS):
+                tiles = slice(2 * pair, 2 * pair + 2)
+                old_t = work.tile([P, 2, FEAT], F32)
+                nc.vector.scalar_tensor_tensor(
+                    out=old_t[:], in0=keep_banks[g, pair][:], scalar=KEEP_FLOOR, in1=c_tiles[g][:, tiles, 0:FEAT],
+                    op0=ALU.add, op1=ALU.mult,
+                )
+                old[pair] = old_t
+            for pair in range(PAIRS):
+                tiles = slice(2 * pair, 2 * pair + 2)
+                gap_t = work.tile([P, 2, FEAT], F32)
+                nc.vector.scalar_tensor_tensor(
+                    out=gap_t[:], in0=cand_tiles[g][:, tiles, :], scalar=1.0 / BETA, in1=old[pair][:],
+                    op0=ALU.mult, op1=ALU.subtract,
+                )
+                gap[pair] = gap_t
+            for pair in range(PAIRS):
+                step_t = work.tile([P, 2, FEAT], F32)
+                nc.vector.tensor_tensor(out=step_t[:], in0=update_banks[g, pair][:], in1=gap[pair][:], op=ALU.mult)
+                step[pair] = step_t
+            for pair in range(PAIRS):
+                tiles = slice(2 * pair, 2 * pair + 2)
+                nc.vector.tensor_tensor(out=m_tile[:, tiles, :], in0=step[pair][:], in1=old[pair][:], op=ALU.add)
+            m_tiles[g] = m_tile
+
+        def row_factors(g):
+            m_sq = stats.tile([P, TILES], F32)
+            unread = work.tile([P, TILES, FEAT], BF16, name="unread_m")
+            for j in range(TILES):
+                nc.scalar.activation(
+                    out=unread[:, j, :], in_=m_tiles[g][:, j, :], func=ACT.Square, accum_out=m_sq[:, j : j + 1]
+                )
+            floored = stats.tile([P, 2 * TILES], F32)
+            nc.gpsimd.tensor_scalar(
+                out=floored[:, 0:TILES], in0=h_sq_tiles[g][:], scalar1=H_SQ_FLOOR, scalar2=None, op0=ALU.max
+            )
+            nc.gpsimd.tensor_scalar(
+                out=floored[:, TILES : 2 * TILES], in0=m_sq[:], scalar1=M_SQ_FLOOR, scalar2=None, op0=ALU.max
+            )
+            roots = stats.tile([P, 2 * TILES], F32)
+            nc.gpsimd.tensor_tensor(out=roots[:], in0=floored[:], in1=exponents[:], op=ALU.pow)
+            factor = stats.tile([P, TILES], F32)
+            nc.gpsimd.tensor_tensor(
+                out=factor[:], in0=roots[:, 0:TILES], in1=roots[:, TILES : 2 * TILES], op=ALU.mult
+            )
+            factor_tiles[g] = factor
+
+        def finish(g):
+            result = rows_out.tile([P, TILES, FEAT], F32)
+            for j in range(TILES):
+                nc.vector.tensor_scalar(
+                    out=result[:, j, :], in0=m_tiles[g][:, j, :], scalar1=factor_tiles[g][:, j : j + 1], scalar2=None,
+                    op0=ALU.mult,
+                )
+            nc.sync.dma_start(out=out_rows[g], in_=result[:])
+
+        load(0)
+
+        warm = const.tile([P, 1], F32)
+        nc.vector.memset(warm[:], 0.0)
+        nc.scalar.activation(out=warm[:], in_=warm[:], func=ACT.Sigmoid)
+
+        identity = const.tile([P, P], F32)
+        make_identity(nc, identity[:])
+        exponents = const.tile([P, 2 * TILES], F32)
+        nc.gpsimd.memset(exponents[:, 0:TILES], 0.5)
+        nc.gpsimd.memset(exponents[:, TILES : 2 * TILES], -0.5)
+
+        w_words = const.tile([P, 2 * FEAT], U32, align_bytes=64)
+        w_plane = const.tile([P, 2 * FEAT], U8, align_bytes=64)
+        nc.vector.memset(w_plane[:].bitcast(I32), 0)
+        bias_rows = const.tile([P, P], BF16)
+        nc.vector.memset(bias_rows[:], 0.0)
+        for first, words, scales in ((0, Wd_words, Wd_scales), (FEAT, Wu_words, Wu_scales)):
+            nc.sync.dma_start(
+                out=w_words[:, first : first + FEAT].bitcast(I32),
+                in_=words.rearrange("g p n t -> (g p) (n t)").bitcast(I32),
+            )
+            for quadrant in range(4):
+                nc.sync.dma_start(
+                    out=w_plane[32 * quadrant : 32 * quadrant + 4, first : first + FEAT].bitcast(I32),
+                    in_=scales[0, 4 * quadrant : 4 * quadrant + 4, :].bitcast(I32),
+                )
+
+        nc.sync.dma_start(out=bias_rows[0:2, :], in_=bd.rearrange("(r c) -> r c", c=P))
+        nc.sync.dma_start(out=bias_rows[2:4, :], in_=bu.rearrange("(r c) -> r c", c=P))
+        bias_rows_f32 = const.tile([P, P], F32)
+        nc.vector.tensor_copy(out=bias_rows_f32[:], in_=bias_rows[:])
+        bias_ps = ct_ps.tile([P, 2, 2, P], F32, name="planes")
+        nc.tensor.transpose(bias_ps[:, 0, 0, :], bias_rows_f32[:], identity[:])
+        bias_cols = const.tile([P, BLOCKS], F32)
+        nc.vector.tensor_scalar(
+            out=bias_cols[:, 0:2], in0=bias_ps[:, 0, 0, 0:2], scalar1=-1.0, scalar2=-SHIFT, op0=ALU.mult, op1=ALU.add
+        )
+        nc.vector.tensor_copy(out=bias_cols[:, 2:4], in_=bias_ps[:, 0, 0, 2:4])
+
+        for g in range(1, FIRST_STEP + LOAD_AHEAD):
+            load(g)
+
+        for t in range(FIRST_STEP, LAST_STEP + 1):
+            if live(t + LOAD_AHEAD):
+                load(t + LOAD_AHEAD)
+            if live(t):
+                gates(t, (0, 1))
+            if live(t + 1):
+                quantise_c(t + 1)
+            if live(t):
+                gates(t, (2, 3))
+                bring_back(t)
+            if live(t - 2):
+                finish(t - 2)
+            if live(t):
+                blend(t)
+            if live(t - 1):
+                row_factors(t - 1)
+            if live(t + 2):
+                h_square_sums(t + 2)

@@ -23,7 +23,6 @@ GROUPS = ROWS // GROUP_ROWS
 PAIRS = TILES // 2
 BLOCKS = 4
 LOAD_AHEAD = 4
-FIRST_STEP = -2
 LAST_STEP = GROUPS + 1
 
 FLOPS = 2 * ROWS * K * 2 * FEAT
@@ -66,7 +65,7 @@ def tile_liquidmemorycell_pb_t_kernel(
 
         c_tiles, cand_tiles, code_tiles, plane_tiles = {}, {}, {}, {}
         gate_tiles, keep_banks, update_banks = {}, {}, {}
-        m_tiles, h_sq_tiles, factor_tiles = {}, {}, {}
+        m_tiles, h_norm_tiles, m_norm_tiles = {}, {}, {}
 
         def load(g):
             c_tile = rows_in.tile([P, TILES, K], BF16)
@@ -76,15 +75,6 @@ def tile_liquidmemorycell_pb_t_kernel(
             nc.sync.dma_start(out=cand[:], in_=cand_rows[g])
             c_tiles[g] = c_tile
             cand_tiles[g] = cand
-
-        def h_square_sums(g):
-            h_sq = stats.tile([P, TILES], F32)
-            unread = work.tile([P, TILES, FEAT], BF16, name="unread_h")
-            for j in range(TILES):
-                nc.scalar.activation(
-                    out=unread[:, j, :], in_=c_tiles[g][:, j, 0:FEAT], func=ACT.Square, accum_out=h_sq[:, j : j + 1]
-                )
-            h_sq_tiles[g] = h_sq
 
         def quantise_c(g):
             c_words = c_tiles[g][:].rearrange("p j k -> p (j k)").bitcast(F32)
@@ -177,34 +167,30 @@ def tile_liquidmemorycell_pb_t_kernel(
                 nc.vector.tensor_tensor(out=m_tile[:, tiles, :], in0=step[pair][:], in1=old[pair][:], op=ALU.add)
             m_tiles[g] = m_tile
 
-        def row_factors(g):
-            m_sq = stats.tile([P, TILES], F32)
-            unread = work.tile([P, TILES, FEAT], BF16, name="unread_m")
+        def root_of_square_sums(rows_of_tile, floor, exponent, label):
+            sq = stats.tile([P, TILES], F32, name=label + "_sq")
+            unread = work.tile([P, TILES, FEAT], BF16, name=label + "_unread")
             for j in range(TILES):
                 nc.scalar.activation(
-                    out=unread[:, j, :], in_=m_tiles[g][:, j, :], func=ACT.Square, accum_out=m_sq[:, j : j + 1]
+                    out=unread[:, j, :], in_=rows_of_tile(j), func=ACT.Square, accum_out=sq[:, j : j + 1]
                 )
-            floored = stats.tile([P, 2 * TILES], F32)
-            nc.gpsimd.tensor_scalar(
-                out=floored[:, 0:TILES], in0=h_sq_tiles[g][:], scalar1=H_SQ_FLOOR, scalar2=None, op0=ALU.max
-            )
-            nc.gpsimd.tensor_scalar(
-                out=floored[:, TILES : 2 * TILES], in0=m_sq[:], scalar1=M_SQ_FLOOR, scalar2=None, op0=ALU.max
-            )
-            roots = stats.tile([P, 2 * TILES], F32)
-            nc.gpsimd.tensor_tensor(out=roots[:], in0=floored[:], in1=exponents[:], op=ALU.pow)
-            factor = stats.tile([P, TILES], F32)
-            nc.gpsimd.tensor_tensor(
-                out=factor[:], in0=roots[:, 0:TILES], in1=roots[:, TILES : 2 * TILES], op=ALU.mult
-            )
-            factor_tiles[g] = factor
+            floored = stats.tile([P, TILES], F32, name=label + "_floored")
+            nc.gpsimd.tensor_scalar(out=floored[:], in0=sq[:], scalar1=floor, scalar2=None, op0=ALU.max)
+            root = stats.tile([P, TILES], F32, name=label + "_root")
+            nc.gpsimd.tensor_tensor(out=root[:], in0=floored[:], in1=exponent[:], op=ALU.pow)
+            return root
+
+        def norms(g):
+            h_norm_tiles[g] = root_of_square_sums(lambda j: c_tiles[g][:, j, 0:FEAT], H_SQ_FLOOR, plus_half, "h")
+            m_norm_tiles[g] = root_of_square_sums(lambda j: m_tiles[g][:, j, :], M_SQ_FLOOR, minus_half, "m")
 
         def finish(g):
             result = rows_out.tile([P, TILES, FEAT], F32)
             for j in range(TILES):
                 nc.vector.tensor_scalar(
-                    out=result[:, j, :], in0=m_tiles[g][:, j, :], scalar1=factor_tiles[g][:, j : j + 1], scalar2=None,
-                    op0=ALU.mult,
+                    out=result[:, j, :], in0=m_tiles[g][:, j, :],
+                    scalar1=m_norm_tiles[g][:, j : j + 1], scalar2=h_norm_tiles[g][:, j : j + 1],
+                    op0=ALU.mult, op1=ALU.mult,
                 )
             nc.sync.dma_start(out=out_rows[g], in_=result[:])
 
@@ -216,9 +202,10 @@ def tile_liquidmemorycell_pb_t_kernel(
 
         identity = const.tile([P, P], F32)
         make_identity(nc, identity[:])
-        exponents = const.tile([P, 2 * TILES], F32)
-        nc.gpsimd.memset(exponents[:, 0:TILES], 0.5)
-        nc.gpsimd.memset(exponents[:, TILES : 2 * TILES], -0.5)
+        plus_half = const.tile([P, TILES], F32)
+        nc.gpsimd.memset(plus_half[:], 0.5)
+        minus_half = const.tile([P, TILES], F32)
+        nc.gpsimd.memset(minus_half[:], -0.5)
 
         w_words = const.tile([P, 2 * FEAT], U32, align_bytes=64)
         w_plane = const.tile([P, 2 * FEAT], U8, align_bytes=64)
@@ -238,8 +225,12 @@ def tile_liquidmemorycell_pb_t_kernel(
 
         nc.sync.dma_start(out=bias_rows[0:2, :], in_=bd.rearrange("(r c) -> r c", c=P))
         nc.sync.dma_start(out=bias_rows[2:4, :], in_=bu.rearrange("(r c) -> r c", c=P))
+        for g in range(1, LOAD_AHEAD):
+            load(g)
+
         bias_rows_f32 = const.tile([P, P], F32)
         nc.vector.tensor_copy(out=bias_rows_f32[:], in_=bias_rows[:])
+        quantise_c(0)
         bias_ps = ct_ps.tile([P, 2, 2, P], F32, name="planes")
         nc.tensor.transpose(bias_ps[:, 0, 0, :], bias_rows_f32[:], identity[:])
         bias_cols = const.tile([P, BLOCKS], F32)
@@ -248,10 +239,7 @@ def tile_liquidmemorycell_pb_t_kernel(
         )
         nc.vector.tensor_copy(out=bias_cols[:, 2:4], in_=bias_ps[:, 0, 0, 2:4])
 
-        for g in range(1, FIRST_STEP + LOAD_AHEAD):
-            load(g)
-
-        for t in range(FIRST_STEP, LAST_STEP + 1):
+        for t in range(LAST_STEP + 1):
             if live(t + LOAD_AHEAD):
                 load(t + LOAD_AHEAD)
             if live(t):
@@ -266,6 +254,4 @@ def tile_liquidmemorycell_pb_t_kernel(
             if live(t):
                 blend(t)
             if live(t - 1):
-                row_factors(t - 1)
-            if live(t + 2):
-                h_square_sums(t + 2)
+                norms(t - 1)

@@ -22,8 +22,12 @@ GROUP_ROWS = TILES * P
 GROUPS = ROWS // GROUP_ROWS
 PAIRS = TILES // 2
 BLOCKS = 4
-LOAD_AHEAD = 4
-LAST_STEP = GROUPS + 1
+KEEP_BLOCKS, UPDATE_BLOCKS = (0, 1), (2, 3)
+LOAD_AHEAD = 6
+TURN_AHEAD = 4
+FIRST_STEP = -TURN_AHEAD
+LAST_STEP = GROUPS
+CAND_BY_PE = range(2, GROUPS - 2)
 
 FLOPS = 2 * ROWS * K * 2 * FEAT
 
@@ -53,34 +57,35 @@ def tile_liquidmemorycell_pb_t_kernel(
     with ExitStack() as stack:
         const = stack.enter_context(tc.tile_pool(name="const", bufs=1))
         rows_in = stack.enter_context(tc.tile_pool(name="rows_in", bufs=LOAD_AHEAD + 2))
-        quant = stack.enter_context(tc.tile_pool(name="quant", bufs=2))
-        gates_sb = stack.enter_context(tc.tile_pool(name="gates_sb", bufs=2))
-        work = stack.enter_context(tc.tile_pool(name="work", bufs=PAIRS))
-        rows_out = stack.enter_context(tc.tile_pool(name="rows_out", bufs=3))
+        quant = stack.enter_context(tc.tile_pool(name="quant", bufs=4))
+        gates_sb = stack.enter_context(tc.tile_pool(name="gates_sb", bufs=3))
+        work = stack.enter_context(tc.tile_pool(name="work", bufs=2 * PAIRS))
+        rows_out = stack.enter_context(tc.tile_pool(name="rows_out", bufs=4))
         stats = stack.enter_context(tc.tile_pool(name="stats", bufs=6))
         ct_ps = stack.enter_context(tc.psum_pool(name="ct_ps", bufs=2))
         sum_ps = stack.enter_context(tc.psum_pool(name="sum_ps", bufs=2))
-        back_ps = stack.enter_context(tc.psum_pool(name="back_ps", bufs=PAIRS))
+        back_ps = stack.enter_context(tc.psum_pool(name="back_ps", bufs=3))
+        cand_ps = stack.enter_context(tc.psum_pool(name="cand_ps", bufs=1))
         stack.enter_context(tc.manual_schedule())
 
-        c_tiles, cand_tiles, code_tiles, plane_tiles = {}, {}, {}, {}
-        gate_tiles, keep_banks, update_banks = {}, {}, {}
-        m_tiles, h_norm_tiles, m_norm_tiles = {}, {}, {}
+        c_tiles, cand_tiles, cand_banks, plane_sets, grouped_tiles, code_tiles, plane_tiles = {}, {}, {}, {}, {}, {}, {}
+        sum_tiles, gate_tiles, keep_banks, update_banks = {}, {}, {}, {}
+        old_tiles, gap_tiles, m_tiles, h_sq_tiles, m_sq_tiles, h_inv_tiles, ratio_tiles, root_tiles = {}, {}, {}, {}, {}, {}, {}, {}
 
-        def load(g):
+        def load_c(g):
             c_tile = rows_in.tile([P, TILES, K], BF16)
             nc.sync.dma_start(out=c_tile[:, :, 0:FEAT], in_=h_rows[g])
             nc.sync.dma_start(out=c_tile[:, :, FEAT:K], in_=x_rows[g])
+            c_tiles[g] = c_tile
+
+        def load_cand(g):
             cand = rows_in.tile([P, TILES, FEAT], BF16)
             nc.sync.dma_start(out=cand[:], in_=cand_rows[g])
-            c_tiles[g] = c_tile
             cand_tiles[g] = cand
 
-        def quantise_c(g):
+        def turn_c(g):
             c_words = c_tiles[g][:].rearrange("p j k -> p (j k)").bitcast(F32)
             words_in_row = K // 2
-            grouped = quant.tile([P, GROUP_ROWS * 4], BF16, align_bytes=64)
-            grouped_words = grouped[:].bitcast(F32).rearrange("p (j b u) -> p j b u", j=TILES, u=2)
             for pair in range(PAIRS):
                 planes = ct_ps.tile([P, 2, 2, P], F32)
                 for jj in range(2):
@@ -89,20 +94,23 @@ def tile_liquidmemorycell_pb_t_kernel(
                         nc.tensor.transpose(
                             planes[:, jj, u, :], c_words[:, first + u : first + words_in_row : 2], identity[:]
                         )
-                nc.scalar.copy(
-                    out=grouped_words[:, 2 * pair : 2 * pair + 2], in_=planes[:].rearrange("p j u b -> p j b u")
-                )
+                plane_sets[g, pair] = planes
+
+        def lay_out_c(g):
+            grouped = quant.tile([P, GROUP_ROWS * 4], BF16, align_bytes=64)
+            grouped_words = grouped[:].bitcast(F32).rearrange("p (j b u) -> p j b u", j=TILES, u=2)
+            nc.scalar.copy(out=grouped_words[:, 0:2], in_=plane_sets[g, 0][:].rearrange("p j u b -> p j b u"))
+            nc.vector.tensor_copy(out=grouped_words[:, 2:4], in_=plane_sets[g, 1][:].rearrange("p j u b -> p j b u"))
+            grouped_tiles[g] = grouped
+
+        def quantise_c(g):
             codes = quant.tile([P, GROUP_ROWS], U32, align_bytes=64)
             plane = quant.tile([P, GROUP_ROWS], U8, align_bytes=64)
-            nc.vector.quantize_mx(out=codes[:].bitcast(FP8X4), scales=plane[:], in_=grouped[:])
+            nc.vector.quantize_mx(out=codes[:].bitcast(FP8X4), scales=plane[:], in_=grouped_tiles[g][:])
             code_tiles[g] = codes
             plane_tiles[g] = plane
 
-        def gates(g, blocks):
-            if g not in gate_tiles:
-                gate_T = gates_sb.tile([P, BLOCKS, GROUP_ROWS], F32)
-                gate_tiles[g] = gate_T
-            sums = {}
+        def multiply(g, blocks):
             for blk in blocks:
                 acc = sum_ps.tile([P, GROUP_ROWS], F32)
                 cols = slice(blk * P, (blk + 1) * P)
@@ -115,86 +123,122 @@ def tile_liquidmemorycell_pb_t_kernel(
                     start=True,
                     stop=True,
                 )
-                sums[blk] = acc
+                sum_tiles[g, blk] = acc
+
+        def sigmoids(g, blocks):
+            if g not in gate_tiles:
+                gate_T = gates_sb.tile([P, BLOCKS, GROUP_ROWS], F32)
+                gate_tiles[g] = gate_T
             for blk in blocks:
                 nc.scalar.activation(
                     out=gate_tiles[g][:, blk, :],
-                    in_=sums[blk][:],
+                    in_=sum_tiles[g, blk][:],
                     func=ACT.Sigmoid,
                     bias=bias_cols[:, blk : blk + 1],
-                    scale=(-1.0 if blk < 2 else 1.0),
+                    scale=(-1.0 if blk in KEEP_BLOCKS else 1.0),
                 )
 
-        def bring_back(g):
-            for first_blk, banks, label in ((0, keep_banks, "keep_ps"), (2, update_banks, "update_ps")):
-                for pair in range(PAIRS):
-                    bank = back_ps.tile([P, 2, FEAT], F32, name=label)
-                    for jj in range(2):
-                        rows = slice((2 * pair + jj) * P, (2 * pair + jj + 1) * P)
-                        for half in range(2):
-                            nc.tensor.transpose(
-                                bank[:, jj, half * P : (half + 1) * P],
-                                gate_tiles[g][:, first_blk + half, rows],
-                                identity[:],
-                            )
-                    banks[g, pair] = bank
+        def bring_back(g, blocks, banks):
+            for pair in range(PAIRS):
+                bank = back_ps.tile([P, 2, FEAT], F32)
+                for jj in range(2):
+                    rows = slice((2 * pair + jj) * P, (2 * pair + jj + 1) * P)
+                    for half, blk in enumerate(blocks):
+                        nc.tensor.transpose(
+                            bank[:, jj, half * P : (half + 1) * P], gate_tiles[g][:, blk, rows], identity[:]
+                        )
+                banks[g, pair] = bank
 
-        def blend(g):
-            m_tile = rows_out.tile([P, TILES, FEAT], F32)
-            old, gap, step = {}, {}, {}
+        def copy_cand(g):
+            if g in CAND_BY_PE:
+                bank = cand_ps.tile([P, TILES, FEAT], BF16)
+                for pair in range(PAIRS):
+                    tiles = slice(2 * pair, 2 * pair + 2)
+                    nc.tensor.matmul(
+                        bank[:, tiles, :], lhsT=identity_bf16[:], rhs=cand_tiles[g][:, tiles, :], start=True, stop=True
+                    )
+                cand_banks[g] = bank
+            else:
+                cand_banks[g] = cand_tiles[g]
+
+        def blend_old(g):
             for pair in range(PAIRS):
                 tiles = slice(2 * pair, 2 * pair + 2)
-                old_t = work.tile([P, 2, FEAT], F32)
+                old = work.tile([P, 2, FEAT], F32)
                 nc.vector.scalar_tensor_tensor(
-                    out=old_t[:], in0=keep_banks[g, pair][:], scalar=KEEP_FLOOR, in1=c_tiles[g][:, tiles, 0:FEAT],
+                    out=old[:], in0=keep_banks[g, pair][:], scalar=KEEP_FLOOR, in1=c_tiles[g][:, tiles, 0:FEAT],
                     op0=ALU.add, op1=ALU.mult,
                 )
-                old[pair] = old_t
+                old_tiles[g, pair] = old
             for pair in range(PAIRS):
                 tiles = slice(2 * pair, 2 * pair + 2)
-                gap_t = work.tile([P, 2, FEAT], F32)
+                gap = work.tile([P, 2, FEAT], F32)
                 nc.vector.scalar_tensor_tensor(
-                    out=gap_t[:], in0=cand_tiles[g][:, tiles, :], scalar=1.0 / BETA, in1=old[pair][:],
+                    out=gap[:], in0=cand_banks[g][:, tiles, :], scalar=1.0 / BETA, in1=old_tiles[g, pair][:],
                     op0=ALU.mult, op1=ALU.subtract,
                 )
-                gap[pair] = gap_t
+                gap_tiles[g, pair] = gap
+
+        def blend_new(g):
+            m_tile = rows_out.tile([P, TILES, FEAT], F32)
             for pair in range(PAIRS):
-                step_t = work.tile([P, 2, FEAT], F32)
-                nc.vector.tensor_tensor(out=step_t[:], in0=update_banks[g, pair][:], in1=gap[pair][:], op=ALU.mult)
-                step[pair] = step_t
-            for pair in range(PAIRS):
-                tiles = slice(2 * pair, 2 * pair + 2)
-                nc.vector.tensor_tensor(out=m_tile[:, tiles, :], in0=step[pair][:], in1=old[pair][:], op=ALU.add)
+                step = work.tile([P, 2, FEAT], F32)
+                nc.vector.tensor_tensor(
+                    out=step[:], in0=update_banks[g, pair][:], in1=gap_tiles[g, pair][:], op=ALU.mult
+                )
+                nc.gpsimd.tensor_tensor(
+                    out=m_tile[:, 2 * pair : 2 * pair + 2, :], in0=step[:], in1=old_tiles[g, pair][:], op=ALU.add
+                )
             m_tiles[g] = m_tile
 
-        def root_of_square_sums(rows_of_tile, floor, exponent, label):
-            sq = stats.tile([P, TILES], F32, name=label + "_sq")
-            unread = work.tile([P, TILES, FEAT], BF16, name=label + "_unread")
+        def square_h(g):
+            sq = stats.tile([P, TILES], F32, name="h_sq")
+            unread = work.tile([P, TILES, FEAT], BF16, name="unread")
             for j in range(TILES):
                 nc.scalar.activation(
-                    out=unread[:, j, :], in_=rows_of_tile(j), func=ACT.Square, accum_out=sq[:, j : j + 1]
+                    out=unread[:, j, :], in_=c_tiles[g][:, j, 0:FEAT], func=ACT.Square, accum_out=sq[:, j : j + 1]
                 )
-            floored = stats.tile([P, TILES], F32, name=label + "_floored")
-            nc.gpsimd.tensor_scalar(out=floored[:], in0=sq[:], scalar1=floor, scalar2=None, op0=ALU.max)
-            root = stats.tile([P, TILES], F32, name=label + "_root")
-            nc.gpsimd.tensor_tensor(out=root[:], in0=floored[:], in1=exponent[:], op=ALU.pow)
-            return root
+            h_sq_tiles[g] = sq
 
-        def norms(g):
-            h_norm_tiles[g] = root_of_square_sums(lambda j: c_tiles[g][:, j, 0:FEAT], H_SQ_FLOOR, plus_half, "h")
-            m_norm_tiles[g] = root_of_square_sums(lambda j: m_tiles[g][:, j, :], M_SQ_FLOOR, minus_half, "m")
+        def square_m(g, pair):
+            if pair == 0:
+                sq = stats.tile([P, TILES], F32, name="m_sq")
+                m_sq_tiles[g] = sq
+            unread = work.tile([P, 2, FEAT], BF16, name="unread_m")
+            for jj in range(2):
+                j = 2 * pair + jj
+                nc.scalar.activation(
+                    out=unread[:, jj, :], in_=m_tiles[g][:, j, :], func=ACT.Square,
+                    accum_out=m_sq_tiles[g][:, j : j + 1],
+                )
+
+        def invert_h(g):
+            floored = stats.tile([P, TILES], F32, name="h_floored")
+            nc.vector.tensor_scalar(out=floored[:], in0=h_sq_tiles[g][:], scalar1=H_SQ_FLOOR, scalar2=None, op0=ALU.max)
+            inv = stats.tile([P, TILES], F32, name="h_inv")
+            nc.vector.reciprocal(out=inv[:], in_=floored[:])
+            h_inv_tiles[g] = inv
+
+        def ratio(g):
+            quotient = stats.tile([P, TILES], F32, name="quotient")
+            nc.vector.scalar_tensor_tensor(
+                out=quotient[:], in0=m_sq_tiles[g][:], scalar=M_SQ_FLOOR, in1=h_inv_tiles[g][:],
+                op0=ALU.max, op1=ALU.mult,
+            )
+            root = stats.tile([P, TILES], F32, name="root")
+            nc.gpsimd.tensor_tensor(out=root[:], in0=quotient[:], in1=minus_half[:], op=ALU.pow)
+            root_tiles[g] = root
 
         def finish(g):
             result = rows_out.tile([P, TILES, FEAT], F32)
             for j in range(TILES):
                 nc.vector.tensor_scalar(
-                    out=result[:, j, :], in0=m_tiles[g][:, j, :],
-                    scalar1=m_norm_tiles[g][:, j : j + 1], scalar2=h_norm_tiles[g][:, j : j + 1],
-                    op0=ALU.mult, op1=ALU.mult,
+                    out=result[:, j, :], in0=m_tiles[g][:, j, :], scalar1=root_tiles[g][:, j : j + 1], scalar2=None,
+                    op0=ALU.mult,
                 )
             nc.sync.dma_start(out=out_rows[g], in_=result[:])
 
-        load(0)
+        load_c(0)
 
         warm = const.tile([P, 1], F32)
         nc.vector.memset(warm[:], 0.0)
@@ -202,16 +246,15 @@ def tile_liquidmemorycell_pb_t_kernel(
 
         identity = const.tile([P, P], F32)
         make_identity(nc, identity[:])
-        plus_half = const.tile([P, TILES], F32)
-        nc.gpsimd.memset(plus_half[:], 0.5)
         minus_half = const.tile([P, TILES], F32)
         nc.gpsimd.memset(minus_half[:], -0.5)
-
         w_words = const.tile([P, 2 * FEAT], U32, align_bytes=64)
         w_plane = const.tile([P, 2 * FEAT], U8, align_bytes=64)
-        nc.vector.memset(w_plane[:].bitcast(I32), 0)
         bias_rows = const.tile([P, P], BF16)
         nc.vector.memset(bias_rows[:], 0.0)
+        nc.vector.memset(w_plane[:].bitcast(I32), 0)
+        nc.sync.dma_start(out=bias_rows[0:2, :], in_=bd.rearrange("(r c) -> r c", c=P))
+        nc.sync.dma_start(out=bias_rows[2:4, :], in_=bu.rearrange("(r c) -> r c", c=P))
         for first, words, scales in ((0, Wd_words, Wd_scales), (FEAT, Wu_words, Wu_scales)):
             nc.sync.dma_start(
                 out=w_words[:, first : first + FEAT].bitcast(I32),
@@ -222,36 +265,58 @@ def tile_liquidmemorycell_pb_t_kernel(
                     out=w_plane[32 * quadrant : 32 * quadrant + 4, first : first + FEAT].bitcast(I32),
                     in_=scales[0, 4 * quadrant : 4 * quadrant + 4, :].bitcast(I32),
                 )
-
-        nc.sync.dma_start(out=bias_rows[0:2, :], in_=bd.rearrange("(r c) -> r c", c=P))
-        nc.sync.dma_start(out=bias_rows[2:4, :], in_=bu.rearrange("(r c) -> r c", c=P))
-        for g in range(1, LOAD_AHEAD):
-            load(g)
-
+        load_c(1)
+        load_cand(0)
+        identity_bf16 = const.tile([P, P], BF16)
+        nc.vector.tensor_copy(out=identity_bf16[:], in_=identity[:])
         bias_rows_f32 = const.tile([P, P], F32)
         nc.vector.tensor_copy(out=bias_rows_f32[:], in_=bias_rows[:])
-        quantise_c(0)
-        bias_ps = ct_ps.tile([P, 2, 2, P], F32, name="planes")
-        nc.tensor.transpose(bias_ps[:, 0, 0, :], bias_rows_f32[:], identity[:])
-        bias_cols = const.tile([P, BLOCKS], F32)
-        nc.vector.tensor_scalar(
-            out=bias_cols[:, 0:2], in0=bias_ps[:, 0, 0, 0:2], scalar1=-1.0, scalar2=-SHIFT, op0=ALU.mult, op1=ALU.add
-        )
-        nc.vector.tensor_copy(out=bias_cols[:, 2:4], in_=bias_ps[:, 0, 0, 2:4])
 
-        for t in range(LAST_STEP + 1):
-            if live(t + LOAD_AHEAD):
-                load(t + LOAD_AHEAD)
+        def turn_biases():
+            bias_ps = ct_ps.tile([P, 2, 2, P], F32, name="planes")
+            nc.tensor.transpose(bias_ps[:, 0, 0, :], bias_rows_f32[:], identity[:])
+            nc.vector.tensor_scalar(
+                out=bias_cols[:, 0:2], in0=bias_ps[:, 0, 0, 0:2], scalar1=-1.0, scalar2=-SHIFT, op0=ALU.mult, op1=ALU.add
+            )
+            nc.vector.tensor_copy(out=bias_cols[:, 2:4], in_=bias_ps[:, 0, 0, 2:4])
+
+        bias_cols = const.tile([P, BLOCKS], F32)
+
+        for t in range(FIRST_STEP, LAST_STEP + 1):
+            if t + LOAD_AHEAD >= 2 and live(t + LOAD_AHEAD):
+                load_c(t + LOAD_AHEAD)
+            if t + LOAD_AHEAD - 1 >= 1 and live(t + LOAD_AHEAD - 1):
+                load_cand(t + LOAD_AHEAD - 1)
             if live(t):
-                gates(t, (0, 1))
-            if live(t + 1):
-                quantise_c(t + 1)
-            if live(t):
-                gates(t, (2, 3))
-                bring_back(t)
-            if live(t - 2):
-                finish(t - 2)
-            if live(t):
-                blend(t)
+                blend_new(t)
             if live(t - 1):
-                norms(t - 1)
+                ratio(t - 1)
+            if live(t + 1):
+                multiply(t + 1, UPDATE_BLOCKS)
+                sigmoids(t + 1, KEEP_BLOCKS)
+                bring_back(t + 1, KEEP_BLOCKS, keep_banks)
+            if live(t + 3):
+                lay_out_c(t + 3)
+            if live(t + 1):
+                sigmoids(t + 1, UPDATE_BLOCKS)
+                copy_cand(t + 1)
+                blend_old(t + 1)
+            if live(t + TURN_AHEAD):
+                turn_c(t + TURN_AHEAD)
+            if t == FIRST_STEP:
+                turn_biases()
+            if live(t):
+                square_m(t, 0)
+            if live(t + 1):
+                square_h(t + 1)
+            if live(t):
+                square_m(t, 1)
+            if live(t + 3):
+                quantise_c(t + 3)
+            if live(t + 2):
+                multiply(t + 2, KEEP_BLOCKS)
+            if live(t + 1):
+                bring_back(t + 1, UPDATE_BLOCKS, update_banks)
+                invert_h(t + 1)
+            if live(t - 1):
+                finish(t - 1)

@@ -26,7 +26,7 @@ KEEP_BLOCKS, UPDATE_BLOCKS = (0, 1), (2, 3)
 LOAD_AHEAD = 6
 TURN_AHEAD = 4
 FIRST_STEP = -TURN_AHEAD
-LAST_STEP = GROUPS
+LAST_STEP = GROUPS + 1
 CAND_BY_PE = range(2, GROUPS - 2)
 
 FLOPS = 2 * ROWS * K * 2 * FEAT
@@ -225,8 +225,11 @@ def tile_liquidmemorycell_pb_t_kernel(
                 out=quotient[:], in0=m_sq_tiles[g][:], scalar=M_SQ_FLOOR, in1=h_inv_tiles[g][:],
                 op0=ALU.max, op1=ALU.mult,
             )
+            ratio_tiles[g] = quotient
+
+        def inverse_root(g):
             root = stats.tile([P, TILES], F32, name="root")
-            nc.gpsimd.tensor_tensor(out=root[:], in0=quotient[:], in1=minus_half[:], op=ALU.pow)
+            nc.gpsimd.tensor_tensor(out=root[:], in0=ratio_tiles[g][:], in1=minus_half[:], op=ALU.pow)
             root_tiles[g] = root
 
         def finish(g):
@@ -287,10 +290,10 @@ def tile_liquidmemorycell_pb_t_kernel(
                 load_c(t + LOAD_AHEAD)
             if t + LOAD_AHEAD - 1 >= 1 and live(t + LOAD_AHEAD - 1):
                 load_cand(t + LOAD_AHEAD - 1)
+            if live(t - 2):
+                inverse_root(t - 2)
             if live(t):
                 blend_new(t)
-            if live(t - 1):
-                ratio(t - 1)
             if live(t + 1):
                 multiply(t + 1, UPDATE_BLOCKS)
                 sigmoids(t + 1, KEEP_BLOCKS)
@@ -305,11 +308,10 @@ def tile_liquidmemorycell_pb_t_kernel(
                 turn_c(t + TURN_AHEAD)
             if t == FIRST_STEP:
                 turn_biases()
-            if live(t):
-                square_m(t, 0)
             if live(t + 1):
                 square_h(t + 1)
             if live(t):
+                square_m(t, 0)
                 square_m(t, 1)
             if live(t + 3):
                 quantise_c(t + 3)
@@ -317,6 +319,9 @@ def tile_liquidmemorycell_pb_t_kernel(
                 multiply(t + 2, KEEP_BLOCKS)
             if live(t + 1):
                 bring_back(t + 1, UPDATE_BLOCKS, update_banks)
-                invert_h(t + 1)
+            if live(t - 2):
+                finish(t - 2)
+            if live(t):
+                invert_h(t)
             if live(t - 1):
-                finish(t - 1)
+                ratio(t - 1)

@@ -23,11 +23,10 @@ GROUPS = ROWS // GROUP_ROWS
 PAIRS = TILES // 2
 BLOCKS = 4
 KEEP_BLOCKS, UPDATE_BLOCKS = (0, 1), (2, 3)
-LOAD_AHEAD = 6
-TURN_AHEAD = 4
-FIRST_STEP = -TURN_AHEAD
-LAST_STEP = GROUPS + 1
-CAND_BY_PE = range(2, GROUPS - 2)
+LAST = GROUPS - 1
+LOAD_AHEAD = 7
+CAND_BY_PE = range(4, GROUPS)
+SCALED_BY_SCALAR = range(11, GROUPS)
 
 FLOPS = 2 * ROWS * K * 2 * FEAT
 
@@ -56,7 +55,7 @@ def tile_liquidmemorycell_pb_t_kernel(
 
     with ExitStack() as stack:
         const = stack.enter_context(tc.tile_pool(name="const", bufs=1))
-        rows_in = stack.enter_context(tc.tile_pool(name="rows_in", bufs=LOAD_AHEAD + 2))
+        rows_in = stack.enter_context(tc.tile_pool(name="rows_in", bufs=LOAD_AHEAD + 1))
         quant = stack.enter_context(tc.tile_pool(name="quant", bufs=4))
         gates_sb = stack.enter_context(tc.tile_pool(name="gates_sb", bufs=3))
         work = stack.enter_context(tc.tile_pool(name="work", bufs=2 * PAIRS))
@@ -186,7 +185,8 @@ def tile_liquidmemorycell_pb_t_kernel(
                 nc.vector.tensor_tensor(
                     out=step[:], in0=update_banks[g, pair][:], in1=gap_tiles[g, pair][:], op=ALU.mult
                 )
-                nc.gpsimd.tensor_tensor(
+                adder = nc.vector if g == LAST else nc.gpsimd
+                adder.tensor_tensor(
                     out=m_tile[:, 2 * pair : 2 * pair + 2, :], in0=step[:], in1=old_tiles[g, pair][:], op=ALU.add
                 )
             m_tiles[g] = m_tile
@@ -235,10 +235,15 @@ def tile_liquidmemorycell_pb_t_kernel(
         def finish(g):
             result = rows_out.tile([P, TILES, FEAT], F32)
             for j in range(TILES):
-                nc.vector.tensor_scalar(
-                    out=result[:, j, :], in0=m_tiles[g][:, j, :], scalar1=root_tiles[g][:, j : j + 1], scalar2=None,
-                    op0=ALU.mult,
-                )
+                if g in SCALED_BY_SCALAR:
+                    nc.scalar.activation(
+                        out=result[:, j, :], in_=m_tiles[g][:, j, :], func=ACT.Copy, scale=root_tiles[g][:, j : j + 1]
+                    )
+                else:
+                    nc.vector.tensor_scalar(
+                        out=result[:, j, :], in0=m_tiles[g][:, j, :], scalar1=root_tiles[g][:, j : j + 1],
+                        scalar2=None, op0=ALU.mult,
+                    )
             nc.sync.dma_start(out=out_rows[g], in_=result[:])
 
         load_c(0)
@@ -256,72 +261,111 @@ def tile_liquidmemorycell_pb_t_kernel(
         bias_rows = const.tile([P, P], BF16)
         nc.vector.memset(bias_rows[:], 0.0)
         nc.vector.memset(w_plane[:].bitcast(I32), 0)
-        nc.sync.dma_start(out=bias_rows[0:2, :], in_=bd.rearrange("(r c) -> r c", c=P))
-        nc.sync.dma_start(out=bias_rows[2:4, :], in_=bu.rearrange("(r c) -> r c", c=P))
-        for first, words, scales in ((0, Wd_words, Wd_scales), (FEAT, Wu_words, Wu_scales)):
+        for first, words in ((0, Wd_words), (FEAT, Wu_words)):
             nc.sync.dma_start(
                 out=w_words[:, first : first + FEAT].bitcast(I32),
                 in_=words.rearrange("g p n t -> (g p) (n t)").bitcast(I32),
             )
+        nc.sync.dma_start(out=bias_rows[0:2, :], in_=bd.rearrange("(r c) -> r c", c=P))
+        nc.sync.dma_start(out=bias_rows[2:4, :], in_=bu.rearrange("(r c) -> r c", c=P))
+        for first, scales in ((0, Wd_scales), (FEAT, Wu_scales)):
             for quadrant in range(4):
                 nc.sync.dma_start(
                     out=w_plane[32 * quadrant : 32 * quadrant + 4, first : first + FEAT].bitcast(I32),
                     in_=scales[0, 4 * quadrant : 4 * quadrant + 4, :].bitcast(I32),
                 )
         load_c(1)
+        load_c(2)
         load_cand(0)
+        load_c(3)
+        for g in range(4, LOAD_AHEAD):
+            load_cand(g - 3)
+            load_c(g)
+
         identity_bf16 = const.tile([P, P], BF16)
         nc.vector.tensor_copy(out=identity_bf16[:], in_=identity[:])
         bias_rows_f32 = const.tile([P, P], F32)
         nc.vector.tensor_copy(out=bias_rows_f32[:], in_=bias_rows[:])
-
-        def turn_biases():
-            bias_ps = ct_ps.tile([P, 2, 2, P], F32, name="planes")
-            nc.tensor.transpose(bias_ps[:, 0, 0, :], bias_rows_f32[:], identity[:])
-            nc.vector.tensor_scalar(
-                out=bias_cols[:, 0:2], in0=bias_ps[:, 0, 0, 0:2], scalar1=-1.0, scalar2=-SHIFT, op0=ALU.mult, op1=ALU.add
-            )
-            nc.vector.tensor_copy(out=bias_cols[:, 2:4], in_=bias_ps[:, 0, 0, 2:4])
-
         bias_cols = const.tile([P, BLOCKS], F32)
 
-        for t in range(FIRST_STEP, LAST_STEP + 1):
-            if t + LOAD_AHEAD >= 2 and live(t + LOAD_AHEAD):
+        turn_c(0)
+        bias_ps = ct_ps.tile([P, 2, 2, P], F32, name="planes")
+        nc.tensor.transpose(bias_ps[:, 0, 0, :], bias_rows_f32[:], identity[:])
+        nc.vector.tensor_scalar(
+            out=bias_cols[:, 0:2], in0=bias_ps[:, 0, 0, 0:2], scalar1=-1.0, scalar2=-SHIFT, op0=ALU.mult, op1=ALU.add
+        )
+        nc.vector.tensor_copy(out=bias_cols[:, 2:4], in_=bias_ps[:, 0, 0, 2:4])
+        lay_out_c(0)
+        quantise_c(0)
+        square_h(0)
+        multiply(0, KEEP_BLOCKS)
+        turn_c(1)
+        sigmoids(0, KEEP_BLOCKS)
+        multiply(0, UPDATE_BLOCKS)
+        lay_out_c(1)
+        bring_back(0, KEEP_BLOCKS, keep_banks)
+        sigmoids(0, UPDATE_BLOCKS)
+        quantise_c(1)
+        bring_back(0, UPDATE_BLOCKS, update_banks)
+        multiply(1, KEEP_BLOCKS)
+        copy_cand(0)
+        blend_old(0)
+        turn_c(2)
+        lay_out_c(2)
+        square_h(1)
+        turn_c(3)
+        quantise_c(2)
+        copy_cand(1)
+
+        for t in range(GROUPS):
+            if live(t + LOAD_AHEAD):
                 load_c(t + LOAD_AHEAD)
-            if t + LOAD_AHEAD - 1 >= 1 and live(t + LOAD_AHEAD - 1):
-                load_cand(t + LOAD_AHEAD - 1)
+            if live(t + LOAD_AHEAD - 3):
+                load_cand(t + LOAD_AHEAD - 3)
             if live(t - 2):
                 inverse_root(t - 2)
-            if live(t):
-                blend_new(t)
-            if live(t + 1):
-                multiply(t + 1, UPDATE_BLOCKS)
+            blend_new(t)
+            if t < LAST - 1:
                 sigmoids(t + 1, KEEP_BLOCKS)
+                multiply(t + 1, UPDATE_BLOCKS)
+            if live(t + 1):
                 bring_back(t + 1, KEEP_BLOCKS, keep_banks)
             if live(t + 3):
                 lay_out_c(t + 3)
-            if live(t + 1):
+            if t < LAST - 1:
                 sigmoids(t + 1, UPDATE_BLOCKS)
-                copy_cand(t + 1)
-                blend_old(t + 1)
-            if live(t + TURN_AHEAD):
-                turn_c(t + TURN_AHEAD)
-            if t == FIRST_STEP:
-                turn_biases()
             if live(t + 1):
-                square_h(t + 1)
-            if live(t):
-                square_m(t, 0)
-                square_m(t, 1)
-            if live(t + 3):
-                quantise_c(t + 3)
-            if live(t + 2):
-                multiply(t + 2, KEEP_BLOCKS)
+                blend_old(t + 1)
+            if live(t + 4):
+                turn_c(t + 4)
             if live(t + 1):
                 bring_back(t + 1, UPDATE_BLOCKS, update_banks)
+            if live(t + 2):
+                square_h(t + 2)
+            if t < LAST - 2:
+                if live(t + 3):
+                    quantise_c(t + 3)
+                multiply(t + 2, KEEP_BLOCKS)
+                copy_cand(t + 2)
+            elif t == LAST - 2:
+                multiply(LAST, KEEP_BLOCKS)
+                copy_cand(LAST)
+                sigmoids(LAST, KEEP_BLOCKS)
+                multiply(LAST, UPDATE_BLOCKS)
+                sigmoids(LAST, UPDATE_BLOCKS)
+            if t == LAST:
+                invert_h(t)
+                ratio(t - 1)
+                inverse_root(t - 1)
+            square_m(t, 0)
+            square_m(t, 1)
             if live(t - 2):
                 finish(t - 2)
-            if live(t):
+            if t < LAST:
                 invert_h(t)
-            if live(t - 1):
-                ratio(t - 1)
+                if live(t - 1):
+                    ratio(t - 1)
+        ratio(LAST)
+        inverse_root(LAST)
+        finish(LAST - 1)
+        finish(LAST)

@@ -26,7 +26,7 @@ KEEP_BLOCKS, UPDATE_BLOCKS = (0, 1), (2, 3)
 LAST = GROUPS - 1
 LOAD_AHEAD = 7
 CAND_BY_PE = range(4, GROUPS)
-SCALED_BY_SCALAR = range(11, GROUPS)
+SCALED_BY_SCALAR = (12, 13)
 
 FLOPS = 2 * ROWS * K * 2 * FEAT
 
@@ -59,8 +59,8 @@ def tile_liquidmemorycell_pb_t_kernel(
         quant = stack.enter_context(tc.tile_pool(name="quant", bufs=4))
         gates_sb = stack.enter_context(tc.tile_pool(name="gates_sb", bufs=3))
         work = stack.enter_context(tc.tile_pool(name="work", bufs=2 * PAIRS))
-        rows_out = stack.enter_context(tc.tile_pool(name="rows_out", bufs=4))
-        stats = stack.enter_context(tc.tile_pool(name="stats", bufs=6))
+        rows_out = stack.enter_context(tc.tile_pool(name="rows_out", bufs=5))
+        stats = stack.enter_context(tc.tile_pool(name="stats", bufs=8))
         ct_ps = stack.enter_context(tc.psum_pool(name="ct_ps", bufs=2))
         sum_ps = stack.enter_context(tc.psum_pool(name="sum_ps", bufs=2))
         back_ps = stack.enter_context(tc.psum_pool(name="back_ps", bufs=3))
@@ -70,6 +70,7 @@ def tile_liquidmemorycell_pb_t_kernel(
         c_tiles, cand_tiles, cand_banks, plane_sets, grouped_tiles, code_tiles, plane_tiles = {}, {}, {}, {}, {}, {}, {}
         sum_tiles, gate_tiles, keep_banks, update_banks = {}, {}, {}, {}
         old_tiles, gap_tiles, m_tiles, h_sq_tiles, m_sq_tiles, h_inv_tiles, ratio_tiles, root_tiles = {}, {}, {}, {}, {}, {}, {}, {}
+        h_floored_tiles = {}
 
         def load_c(g):
             c_tile = rows_in.tile([P, TILES, K], BF16)
@@ -82,10 +83,10 @@ def tile_liquidmemorycell_pb_t_kernel(
             nc.sync.dma_start(out=cand[:], in_=cand_rows[g])
             cand_tiles[g] = cand
 
-        def turn_c(g):
+        def turn_c(g, pairs=(0, 1)):
             c_words = c_tiles[g][:].rearrange("p j k -> p (j k)").bitcast(F32)
             words_in_row = K // 2
-            for pair in range(PAIRS):
+            for pair in pairs:
                 planes = ct_ps.tile([P, 2, 2, P], F32)
                 for jj in range(2):
                     first = (2 * pair + jj) * words_in_row
@@ -148,17 +149,17 @@ def tile_liquidmemorycell_pb_t_kernel(
                         )
                 banks[g, pair] = bank
 
-        def copy_cand(g):
-            if g in CAND_BY_PE:
-                bank = cand_ps.tile([P, TILES, FEAT], BF16)
-                for pair in range(PAIRS):
-                    tiles = slice(2 * pair, 2 * pair + 2)
-                    nc.tensor.matmul(
-                        bank[:, tiles, :], lhsT=identity_bf16[:], rhs=cand_tiles[g][:, tiles, :], start=True, stop=True
-                    )
-                cand_banks[g] = bank
-            else:
+        def copy_cand(g, pair):
+            if g not in CAND_BY_PE:
                 cand_banks[g] = cand_tiles[g]
+                return
+            if pair == 0:
+                bank = cand_ps.tile([P, TILES, FEAT], BF16)
+                cand_banks[g] = bank
+            tiles = slice(2 * pair, 2 * pair + 2)
+            nc.tensor.matmul(
+                cand_banks[g][:, tiles, :], lhsT=identity_bf16[:], rhs=cand_tiles[g][:, tiles, :], start=True, stop=True
+            )
 
         def blend_old(g):
             for pair in range(PAIRS):
@@ -212,11 +213,14 @@ def tile_liquidmemorycell_pb_t_kernel(
                     accum_out=m_sq_tiles[g][:, j : j + 1],
                 )
 
-        def invert_h(g):
+        def floor_h(g):
             floored = stats.tile([P, TILES], F32, name="h_floored")
             nc.vector.tensor_scalar(out=floored[:], in0=h_sq_tiles[g][:], scalar1=H_SQ_FLOOR, scalar2=None, op0=ALU.max)
+            h_floored_tiles[g] = floored
+
+        def invert_h(g):
             inv = stats.tile([P, TILES], F32, name="h_inv")
-            nc.vector.reciprocal(out=inv[:], in_=floored[:])
+            nc.vector.reciprocal(out=inv[:], in_=h_floored_tiles[g][:])
             h_inv_tiles[g] = inv
 
         def ratio(g):
@@ -308,23 +312,23 @@ def tile_liquidmemorycell_pb_t_kernel(
         quantise_c(1)
         bring_back(0, UPDATE_BLOCKS, update_banks)
         multiply(1, KEEP_BLOCKS)
-        copy_cand(0)
+        copy_cand(0, 0)
         blend_old(0)
         turn_c(2)
         lay_out_c(2)
         square_h(1)
         turn_c(3)
         quantise_c(2)
-        copy_cand(1)
+        copy_cand(1, 0)
 
         for t in range(GROUPS):
             if live(t + LOAD_AHEAD):
                 load_c(t + LOAD_AHEAD)
             if live(t + LOAD_AHEAD - 3):
                 load_cand(t + LOAD_AHEAD - 3)
+            blend_new(t)
             if live(t - 2):
                 inverse_root(t - 2)
-            blend_new(t)
             if t < LAST - 1:
                 sigmoids(t + 1, KEEP_BLOCKS)
                 multiply(t + 1, UPDATE_BLOCKS)
@@ -334,37 +338,43 @@ def tile_liquidmemorycell_pb_t_kernel(
                 lay_out_c(t + 3)
             if t < LAST - 1:
                 sigmoids(t + 1, UPDATE_BLOCKS)
+            if live(t + 4):
+                turn_c(t + 4, (0,))
+            if t < LAST - 2:
+                multiply(t + 2, (0,))
+            if live(t + 1):
+                copy_cand(t + 1, 1)
+            if live(t + 4):
+                turn_c(t + 4, (1,))
             if live(t + 1):
                 blend_old(t + 1)
-            if live(t + 4):
-                turn_c(t + 4)
-            if live(t + 1):
                 bring_back(t + 1, UPDATE_BLOCKS, update_banks)
-            if live(t + 2):
-                square_h(t + 2)
             if t < LAST - 2:
-                if live(t + 3):
-                    quantise_c(t + 3)
-                multiply(t + 2, KEEP_BLOCKS)
-                copy_cand(t + 2)
+                multiply(t + 2, (1,))
             elif t == LAST - 2:
                 multiply(LAST, KEEP_BLOCKS)
-                copy_cand(LAST)
                 sigmoids(LAST, KEEP_BLOCKS)
                 multiply(LAST, UPDATE_BLOCKS)
                 sigmoids(LAST, UPDATE_BLOCKS)
-            if t == LAST:
-                invert_h(t)
+            if live(t + 2):
+                copy_cand(t + 2, 0)
+            if live(t - 1):
+                square_m(t - 1, 0)
+                square_m(t - 1, 1)
+            if live(t + 2):
+                square_h(t + 2)
+            if live(t + 3):
+                quantise_c(t + 3)
+            floor_h(t)
+            if live(t - 3):
+                finish(t - 3)
+            invert_h(t)
+            if live(t - 1):
                 ratio(t - 1)
-                inverse_root(t - 1)
-            square_m(t, 0)
-            square_m(t, 1)
-            if live(t - 2):
-                finish(t - 2)
-            if t < LAST:
-                invert_h(t)
-                if live(t - 1):
-                    ratio(t - 1)
+        inverse_root(LAST - 1)
+        square_m(LAST, 0)
+        square_m(LAST, 1)
+        finish(LAST - 2)
         ratio(LAST)
         inverse_root(LAST)
         finish(LAST - 1)

@@ -110,19 +110,20 @@ def tile_liquidmemorycell_pb_t_kernel(
             code_tiles[g] = codes
             plane_tiles[g] = plane
 
-        def multiply(g, blocks):
+        def multiply(g, blocks, times=1):
             for blk in blocks:
                 acc = sum_ps.tile([P, GROUP_ROWS], F32)
                 cols = slice(blk * P, (blk + 1) * P)
-                nc.tensor.matmul_mx(
-                    out=acc[:],
-                    lhsT=w_words[:, cols].bitcast(FP8X4),
-                    lhsT_scale=w_plane[:, cols],
-                    rhs=code_tiles[g][:].bitcast(FP8X4),
-                    rhs_scale=plane_tiles[g][:],
-                    start=True,
-                    stop=True,
-                )
+                for pass_no in range(times):
+                    nc.tensor.matmul_mx(
+                        out=acc[:],
+                        lhsT=w_words[:, cols].bitcast(FP8X4),
+                        lhsT_scale=w_plane[:, cols],
+                        rhs=code_tiles[g][:].bitcast(FP8X4),
+                        rhs_scale=plane_tiles[g][:],
+                        start=True,
+                        stop=True,
+                    )
                 sum_tiles[g, blk] = acc
 
         def sigmoids(g, blocks):
@@ -338,29 +339,28 @@ def tile_liquidmemorycell_pb_t_kernel(
                 lay_out_c(t + 3)
             if t < LAST - 1:
                 sigmoids(t + 1, UPDATE_BLOCKS)
-            if live(t + 4):
-                turn_c(t + 4, (0,))
             if t < LAST - 2:
-                multiply(t + 2, (0,))
+                multiply(t + 2, (0,), times=2)
             if live(t + 1):
                 copy_cand(t + 1, 1)
             if live(t + 4):
-                turn_c(t + 4, (1,))
+                turn_c(t + 4)
             if live(t + 1):
                 blend_old(t + 1)
-                bring_back(t + 1, UPDATE_BLOCKS, update_banks)
             if t < LAST - 2:
-                multiply(t + 2, (1,))
-            elif t == LAST - 2:
+                multiply(t + 2, (1,), times=2)
+            if live(t + 1):
+                bring_back(t + 1, UPDATE_BLOCKS, update_banks)
+            if live(t - 1):
+                square_m(t - 1, 0)
+                square_m(t - 1, 1)
+            if t == LAST - 2:
                 multiply(LAST, KEEP_BLOCKS)
                 sigmoids(LAST, KEEP_BLOCKS)
                 multiply(LAST, UPDATE_BLOCKS)
                 sigmoids(LAST, UPDATE_BLOCKS)
             if live(t + 2):
                 copy_cand(t + 2, 0)
-            if live(t - 1):
-                square_m(t - 1, 0)
-                square_m(t - 1, 1)
             if live(t + 2):
                 square_h(t + 2)
             if live(t + 3):

@@ -24,9 +24,11 @@ PAIRS = TILES // 2
 BLOCKS = 4
 KEEP_BLOCKS, UPDATE_BLOCKS = (0, 1), (2, 3)
 LAST = GROUPS - 1
+WARM_MATMULS = 3
+SQUARED_BY_VECTOR = (1,)
 LOAD_AHEAD = 7
 CAND_BY_PE = range(4, GROUPS)
-SCALED_BY_SCALAR = (12, 13)
+SCALED_BY_SCALAR = {12: (0, 1, 2, 3), 13: (0, 1)}
 
 FLOPS = 2 * ROWS * K * 2 * FEAT
 
@@ -70,18 +72,31 @@ def tile_liquidmemorycell_pb_t_kernel(
         c_tiles, cand_tiles, cand_banks, plane_sets, grouped_tiles, code_tiles, plane_tiles = {}, {}, {}, {}, {}, {}, {}
         sum_tiles, gate_tiles, keep_banks, update_banks = {}, {}, {}, {}
         old_tiles, gap_tiles, m_tiles, h_sq_tiles, m_sq_tiles, h_inv_tiles, ratio_tiles, root_tiles = {}, {}, {}, {}, {}, {}, {}, {}
-        h_floored_tiles = {}
+        h_floored_tiles, result_tiles = {}, {}
 
-        def load_c(g):
+        def load_c(g, tiles_at_once=TILES):
             c_tile = rows_in.tile([P, TILES, K], BF16)
-            nc.sync.dma_start(out=c_tile[:, :, 0:FEAT], in_=h_rows[g])
-            nc.sync.dma_start(out=c_tile[:, :, FEAT:K], in_=x_rows[g])
+            for first in range(0, TILES, tiles_at_once):
+                tiles = slice(first, first + tiles_at_once)
+                nc.sync.dma_start(out=c_tile[:, tiles, 0:FEAT], in_=h_rows[g][:, tiles, :])
+                nc.sync.dma_start(out=c_tile[:, tiles, FEAT:K], in_=x_rows[g][:, tiles, :])
             c_tiles[g] = c_tile
 
         def load_cand(g):
             cand = rows_in.tile([P, TILES, FEAT], BF16)
             nc.sync.dma_start(out=cand[:], in_=cand_rows[g])
             cand_tiles[g] = cand
+
+        def load_weight(first, words, scales):
+            cols = slice(first, first + FEAT)
+            nc.sync.dma_start(
+                out=w_words[:, cols].bitcast(I32), in_=words.rearrange("g p n t -> (g p) (n t)").bitcast(I32)
+            )
+            for quadrant in range(4):
+                nc.sync.dma_start(
+                    out=w_plane[32 * quadrant : 32 * quadrant + 4, cols].bitcast(I32),
+                    in_=scales[0, 4 * quadrant : 4 * quadrant + 4, :].bitcast(I32),
+                )
 
         def turn_c(g, pairs=(0, 1)):
             c_words = c_tiles[g][:].rearrange("p j k -> p (j k)").bitcast(F32)
@@ -110,20 +125,19 @@ def tile_liquidmemorycell_pb_t_kernel(
             code_tiles[g] = codes
             plane_tiles[g] = plane
 
-        def multiply(g, blocks, times=1):
+        def multiply(g, blocks):
             for blk in blocks:
                 acc = sum_ps.tile([P, GROUP_ROWS], F32)
                 cols = slice(blk * P, (blk + 1) * P)
-                for pass_no in range(times):
-                    nc.tensor.matmul_mx(
-                        out=acc[:],
-                        lhsT=w_words[:, cols].bitcast(FP8X4),
-                        lhsT_scale=w_plane[:, cols],
-                        rhs=code_tiles[g][:].bitcast(FP8X4),
-                        rhs_scale=plane_tiles[g][:],
-                        start=True,
-                        stop=True,
-                    )
+                nc.tensor.matmul_mx(
+                    out=acc[:],
+                    lhsT=w_words[:, cols].bitcast(FP8X4),
+                    lhsT_scale=w_plane[:, cols],
+                    rhs=code_tiles[g][:].bitcast(FP8X4),
+                    rhs_scale=plane_tiles[g][:],
+                    start=True,
+                    stop=True,
+                )
                 sum_tiles[g, blk] = acc
 
         def sigmoids(g, blocks):
@@ -163,44 +177,56 @@ def tile_liquidmemorycell_pb_t_kernel(
             )
 
         def blend_old(g):
+            old = work.tile([P, TILES, FEAT], F32)
             for pair in range(PAIRS):
                 tiles = slice(2 * pair, 2 * pair + 2)
-                old = work.tile([P, 2, FEAT], F32)
                 nc.vector.scalar_tensor_tensor(
-                    out=old[:], in0=keep_banks[g, pair][:], scalar=KEEP_FLOOR, in1=c_tiles[g][:, tiles, 0:FEAT],
-                    op0=ALU.add, op1=ALU.mult,
+                    out=old[:, tiles, :], in0=keep_banks[g, pair][:], scalar=KEEP_FLOOR,
+                    in1=c_tiles[g][:, tiles, 0:FEAT], op0=ALU.add, op1=ALU.mult,
                 )
-                old_tiles[g, pair] = old
+            gap = work.tile([P, TILES, FEAT], F32)
             for pair in range(PAIRS):
                 tiles = slice(2 * pair, 2 * pair + 2)
-                gap = work.tile([P, 2, FEAT], F32)
                 nc.vector.scalar_tensor_tensor(
-                    out=gap[:], in0=cand_banks[g][:, tiles, :], scalar=1.0 / BETA, in1=old_tiles[g, pair][:],
+                    out=gap[:, tiles, :], in0=cand_banks[g][:, tiles, :], scalar=1.0 / BETA, in1=old[:, tiles, :],
                     op0=ALU.mult, op1=ALU.subtract,
                 )
-                gap_tiles[g, pair] = gap
+            old_tiles[g] = old
+            gap_tiles[g] = gap
 
-        def blend_new(g):
-            m_tile = rows_out.tile([P, TILES, FEAT], F32)
-            for pair in range(PAIRS):
+        def blend_new(g, pairs=(0, 1)):
+            if pairs[0] == 0:
+                m_tile = rows_out.tile([P, TILES, FEAT], F32)
+                m_tiles[g] = m_tile
+            for pair in pairs:
+                tiles = slice(2 * pair, 2 * pair + 2)
                 step = work.tile([P, 2, FEAT], F32)
                 nc.vector.tensor_tensor(
-                    out=step[:], in0=update_banks[g, pair][:], in1=gap_tiles[g, pair][:], op=ALU.mult
+                    out=step[:], in0=update_banks[g, pair][:], in1=gap_tiles[g][:, tiles, :], op=ALU.mult
                 )
                 adder = nc.vector if g == LAST else nc.gpsimd
                 adder.tensor_tensor(
-                    out=m_tile[:, 2 * pair : 2 * pair + 2, :], in0=step[:], in1=old_tiles[g, pair][:], op=ALU.add
+                    out=m_tiles[g][:, tiles, :], in0=step[:], in1=old_tiles[g][:, tiles, :], op=ALU.add
                 )
-            m_tiles[g] = m_tile
 
         def square_h(g):
-            sq = stats.tile([P, TILES], F32, name="h_sq")
+            if g % 2 == 0:
+                sq = stats.tile([P, 2, TILES], F32, name="h_sq")
+                h_sq_tiles[g] = sq
+                h_sq_tiles[g + 1] = sq
             unread = work.tile([P, TILES, FEAT], BF16, name="unread")
             for j in range(TILES):
-                nc.scalar.activation(
-                    out=unread[:, j, :], in_=c_tiles[g][:, j, 0:FEAT], func=ACT.Square, accum_out=sq[:, j : j + 1]
-                )
-            h_sq_tiles[g] = sq
+                h_row = c_tiles[g][:, j, 0:FEAT]
+                if g in SQUARED_BY_VECTOR:
+                    nc.vector.scalar_tensor_tensor(
+                        out=unread[:, j, :], in0=h_row, scalar=1.0, in1=h_row, op0=ALU.mult, op1=ALU.mult,
+                        accum_out=h_sq_tiles[g][:, g % 2, j : j + 1],
+                    )
+                else:
+                    nc.scalar.activation(
+                        out=unread[:, j, :], in_=h_row, func=ACT.Square,
+                        accum_out=h_sq_tiles[g][:, g % 2, j : j + 1],
+                    )
 
         def square_m(g, pair):
             if pair == 0:
@@ -215,32 +241,40 @@ def tile_liquidmemorycell_pb_t_kernel(
                 )
 
         def floor_h(g):
-            floored = stats.tile([P, TILES], F32, name="h_floored")
+            floored = stats.tile([P, 2, TILES], F32, name="h_floored")
             nc.vector.tensor_scalar(out=floored[:], in0=h_sq_tiles[g][:], scalar1=H_SQ_FLOOR, scalar2=None, op0=ALU.max)
             h_floored_tiles[g] = floored
 
         def invert_h(g):
-            inv = stats.tile([P, TILES], F32, name="h_inv")
+            inv = stats.tile([P, 2, TILES], F32, name="h_inv")
             nc.vector.reciprocal(out=inv[:], in_=h_floored_tiles[g][:])
-            h_inv_tiles[g] = inv
+            h_inv_tiles[g] = inv[:, 0, :]
+            h_inv_tiles[g + 1] = inv[:, 1, :]
 
-        def ratio(g):
-            quotient = stats.tile([P, TILES], F32, name="quotient")
+        def ratio(g, cols=slice(0, TILES)):
+            if cols.start == 0:
+                quotient = stats.tile([P, TILES], F32, name="quotient")
+                ratio_tiles[g] = quotient
             nc.vector.scalar_tensor_tensor(
-                out=quotient[:], in0=m_sq_tiles[g][:], scalar=M_SQ_FLOOR, in1=h_inv_tiles[g][:],
-                op0=ALU.max, op1=ALU.mult,
+                out=ratio_tiles[g][:, cols], in0=m_sq_tiles[g][:, cols], scalar=M_SQ_FLOOR,
+                in1=h_inv_tiles[g][:, cols], op0=ALU.max, op1=ALU.mult,
             )
-            ratio_tiles[g] = quotient
 
-        def inverse_root(g):
-            root = stats.tile([P, TILES], F32, name="root")
-            nc.gpsimd.tensor_tensor(out=root[:], in0=ratio_tiles[g][:], in1=minus_half[:], op=ALU.pow)
-            root_tiles[g] = root
+        def inverse_root(g, cols=slice(0, TILES)):
+            if cols.start == 0:
+                root = stats.tile([P, TILES], F32, name="root")
+                root_tiles[g] = root
+            nc.gpsimd.tensor_tensor(
+                out=root_tiles[g][:, cols], in0=ratio_tiles[g][:, cols], in1=minus_half[:, cols], op=ALU.pow
+            )
 
-        def finish(g):
-            result = rows_out.tile([P, TILES, FEAT], F32)
-            for j in range(TILES):
-                if g in SCALED_BY_SCALAR:
+        def finish(g, tiles=slice(0, TILES)):
+            if tiles.start == 0:
+                result = rows_out.tile([P, TILES, FEAT], F32)
+                result_tiles[g] = result
+            result = result_tiles[g]
+            for j in range(tiles.start, tiles.stop):
+                if j in SCALED_BY_SCALAR.get(g, ()):
                     nc.scalar.activation(
                         out=result[:, j, :], in_=m_tiles[g][:, j, :], func=ACT.Copy, scale=root_tiles[g][:, j : j + 1]
                     )
@@ -249,9 +283,9 @@ def tile_liquidmemorycell_pb_t_kernel(
                         out=result[:, j, :], in0=m_tiles[g][:, j, :], scalar1=root_tiles[g][:, j : j + 1],
                         scalar2=None, op0=ALU.mult,
                     )
-            nc.sync.dma_start(out=out_rows[g], in_=result[:])
+            nc.sync.dma_start(out=out_rows[g][:, tiles, :], in_=result[:, tiles, :])
 
-        load_c(0)
+        load_c(0, tiles_at_once=2)
 
         warm = const.tile([P, 1], F32)
         nc.vector.memset(warm[:], 0.0)
@@ -266,20 +300,11 @@ def tile_liquidmemorycell_pb_t_kernel(
         bias_rows = const.tile([P, P], BF16)
         nc.vector.memset(bias_rows[:], 0.0)
         nc.vector.memset(w_plane[:].bitcast(I32), 0)
-        for first, words in ((0, Wd_words), (FEAT, Wu_words)):
-            nc.sync.dma_start(
-                out=w_words[:, first : first + FEAT].bitcast(I32),
-                in_=words.rearrange("g p n t -> (g p) (n t)").bitcast(I32),
-            )
         nc.sync.dma_start(out=bias_rows[0:2, :], in_=bd.rearrange("(r c) -> r c", c=P))
         nc.sync.dma_start(out=bias_rows[2:4, :], in_=bu.rearrange("(r c) -> r c", c=P))
-        for first, scales in ((0, Wd_scales), (FEAT, Wu_scales)):
-            for quadrant in range(4):
-                nc.sync.dma_start(
-                    out=w_plane[32 * quadrant : 32 * quadrant + 4, first : first + FEAT].bitcast(I32),
-                    in_=scales[0, 4 * quadrant : 4 * quadrant + 4, :].bitcast(I32),
-                )
+        load_weight(0, Wd_words, Wd_scales)
         load_c(1)
+        load_weight(FEAT, Wu_words, Wu_scales)
         load_c(2)
         load_cand(0)
         load_c(3)
@@ -290,19 +315,33 @@ def tile_liquidmemorycell_pb_t_kernel(
         identity_bf16 = const.tile([P, P], BF16)
         nc.vector.tensor_copy(out=identity_bf16[:], in_=identity[:])
         bias_rows_f32 = const.tile([P, P], F32)
-        nc.vector.tensor_copy(out=bias_rows_f32[:], in_=bias_rows[:])
         bias_cols = const.tile([P, BLOCKS], F32)
 
+        warm_ps = back_ps.tile([P, 2, FEAT], F32, name="bank")
+
+        def warm_up(part):
+            nc.tensor.matmul(
+                warm_ps[:, part // 2 % 2, part % 2 * P : (part % 2 + 1) * P], lhsT=identity[:], rhs=identity[:],
+                start=True, stop=True,
+            )
+
+        for part in range(WARM_MATMULS):
+            warm_up(part)
+
         turn_c(0)
+        for part in range(WARM_MATMULS):
+            warm_up(part)
+        lay_out_c(0)
+        nc.vector.tensor_copy(out=bias_rows_f32[:], in_=bias_rows[:])
         bias_ps = ct_ps.tile([P, 2, 2, P], F32, name="planes")
         nc.tensor.transpose(bias_ps[:, 0, 0, :], bias_rows_f32[:], identity[:])
+        quantise_c(0)
         nc.vector.tensor_scalar(
             out=bias_cols[:, 0:2], in0=bias_ps[:, 0, 0, 0:2], scalar1=-1.0, scalar2=-SHIFT, op0=ALU.mult, op1=ALU.add
         )
         nc.vector.tensor_copy(out=bias_cols[:, 2:4], in_=bias_ps[:, 0, 0, 2:4])
-        lay_out_c(0)
-        quantise_c(0)
         square_h(0)
+        square_h(1)
         multiply(0, KEEP_BLOCKS)
         turn_c(1)
         sigmoids(0, KEEP_BLOCKS)
@@ -311,18 +350,17 @@ def tile_liquidmemorycell_pb_t_kernel(
         bring_back(0, KEEP_BLOCKS, keep_banks)
         sigmoids(0, UPDATE_BLOCKS)
         quantise_c(1)
-        bring_back(0, UPDATE_BLOCKS, update_banks)
+        turn_c(2)
         multiply(1, KEEP_BLOCKS)
+        bring_back(0, UPDATE_BLOCKS, update_banks)
         copy_cand(0, 0)
         blend_old(0)
-        turn_c(2)
         lay_out_c(2)
-        square_h(1)
         turn_c(3)
         quantise_c(2)
         copy_cand(1, 0)
 
-        for t in range(GROUPS):
+        for t in range(LAST):
             if live(t + LOAD_AHEAD):
                 load_c(t + LOAD_AHEAD)
             if live(t + LOAD_AHEAD - 3):
@@ -333,24 +371,20 @@ def tile_liquidmemorycell_pb_t_kernel(
             if t < LAST - 1:
                 sigmoids(t + 1, KEEP_BLOCKS)
                 multiply(t + 1, UPDATE_BLOCKS)
-            if live(t + 1):
-                bring_back(t + 1, KEEP_BLOCKS, keep_banks)
+            bring_back(t + 1, KEEP_BLOCKS, keep_banks)
             if live(t + 3):
                 lay_out_c(t + 3)
             if t < LAST - 1:
                 sigmoids(t + 1, UPDATE_BLOCKS)
             if t < LAST - 2:
-                multiply(t + 2, (0,), times=2)
-            if live(t + 1):
-                copy_cand(t + 1, 1)
+                multiply(t + 2, (0,))
+            copy_cand(t + 1, 1)
             if live(t + 4):
                 turn_c(t + 4)
-            if live(t + 1):
-                blend_old(t + 1)
+            blend_old(t + 1)
             if t < LAST - 2:
-                multiply(t + 2, (1,), times=2)
-            if live(t + 1):
-                bring_back(t + 1, UPDATE_BLOCKS, update_banks)
+                multiply(t + 2, (1,))
+            bring_back(t + 1, UPDATE_BLOCKS, update_banks)
             if live(t - 1):
                 square_m(t - 1, 0)
                 square_m(t - 1, 1)
@@ -365,17 +399,31 @@ def tile_liquidmemorycell_pb_t_kernel(
                 square_h(t + 2)
             if live(t + 3):
                 quantise_c(t + 3)
-            floor_h(t)
+            if t % 2 == 0:
+                floor_h(t)
             if live(t - 3):
                 finish(t - 3)
-            invert_h(t)
+            if t % 2 == 0:
+                invert_h(t)
             if live(t - 1):
                 ratio(t - 1)
+
+        first_pair, second_pair = slice(0, 2), slice(2, TILES)
+        blend_new(LAST, (0,))
+        inverse_root(LAST - 2)
+        square_m(LAST - 1, 0)
+        square_m(LAST - 1, 1)
+        ratio(LAST - 1)
         inverse_root(LAST - 1)
+        finish(LAST - 3)
+        blend_new(LAST, (1,))
         square_m(LAST, 0)
+        ratio(LAST, first_pair)
+        inverse_root(LAST, first_pair)
         square_m(LAST, 1)
         finish(LAST - 2)
-        ratio(LAST)
-        inverse_root(LAST)
         finish(LAST - 1)
-        finish(LAST)
+        ratio(LAST, second_pair)
+        inverse_root(LAST, second_pair)
+        finish(LAST, first_pair)
+        finish(LAST, second_pair)

@@ -28,7 +28,7 @@ WARM_MATMULS = 3
 SQUARED_BY_VECTOR = (1,)
 LOAD_AHEAD = 7
 CAND_BY_PE = range(4, GROUPS)
-SCALED_BY_SCALAR = {12: (0, 1, 2, 3), 13: (0, 1)}
+SCALED_BY_SCALAR = {12: (0, 1)}
 
 FLOPS = 2 * ROWS * K * 2 * FEAT
 
@@ -314,7 +314,6 @@ def tile_liquidmemorycell_pb_t_kernel(
 
         identity_bf16 = const.tile([P, P], BF16)
         nc.vector.tensor_copy(out=identity_bf16[:], in_=identity[:])
-        bias_rows_f32 = const.tile([P, P], F32)
         bias_cols = const.tile([P, BLOCKS], F32)
 
         warm_ps = back_ps.tile([P, 2, FEAT], F32, name="bank")
@@ -332,14 +331,13 @@ def tile_liquidmemorycell_pb_t_kernel(
         for part in range(WARM_MATMULS):
             warm_up(part)
         lay_out_c(0)
-        nc.vector.tensor_copy(out=bias_rows_f32[:], in_=bias_rows[:])
-        bias_ps = ct_ps.tile([P, 2, 2, P], F32, name="planes")
-        nc.tensor.transpose(bias_ps[:, 0, 0, :], bias_rows_f32[:], identity[:])
+        bias_ps = ct_ps.tile([P, P], BF16, name="planes")
+        nc.tensor.transpose(bias_ps[:], bias_rows[:], identity_bf16[:])
         quantise_c(0)
         nc.vector.tensor_scalar(
-            out=bias_cols[:, 0:2], in0=bias_ps[:, 0, 0, 0:2], scalar1=-1.0, scalar2=-SHIFT, op0=ALU.mult, op1=ALU.add
+            out=bias_cols[:, 0:2], in0=bias_ps[:, 0:2], scalar1=-1.0, scalar2=-SHIFT, op0=ALU.mult, op1=ALU.add
         )
-        nc.vector.tensor_copy(out=bias_cols[:, 2:4], in_=bias_ps[:, 0, 0, 2:4])
+        nc.vector.tensor_copy(out=bias_cols[:, 2:4], in_=bias_ps[:, 2:4])
         square_h(0)
         square_h(1)
         multiply(0, KEEP_BLOCKS)
@@ -356,7 +354,6 @@ def tile_liquidmemorycell_pb_t_kernel(
         copy_cand(0, 0)
         blend_old(0)
         lay_out_c(2)
-        turn_c(3)
         quantise_c(2)
         copy_cand(1, 0)
 
@@ -371,11 +368,15 @@ def tile_liquidmemorycell_pb_t_kernel(
             if t < LAST - 1:
                 sigmoids(t + 1, KEEP_BLOCKS)
                 multiply(t + 1, UPDATE_BLOCKS)
+            if t == 0:
+                turn_c(3)
             bring_back(t + 1, KEEP_BLOCKS, keep_banks)
-            if live(t + 3):
+            if 0 < t and live(t + 3):
                 lay_out_c(t + 3)
             if t < LAST - 1:
                 sigmoids(t + 1, UPDATE_BLOCKS)
+            if t == 0:
+                lay_out_c(3)
             if t < LAST - 2:
                 multiply(t + 2, (0,))
             copy_cand(t + 1, 1)
@@ -422,8 +423,8 @@ def tile_liquidmemorycell_pb_t_kernel(
         inverse_root(LAST, first_pair)
         square_m(LAST, 1)
         finish(LAST - 2)
-        finish(LAST - 1)
         ratio(LAST, second_pair)
         inverse_root(LAST, second_pair)
+        finish(LAST - 1)
         finish(LAST, first_pair)
         finish(LAST, second_pair)

@@ -25,6 +25,7 @@ BLOCKS = 4
 KEEP_BLOCKS, UPDATE_BLOCKS = (0, 1), (2, 3)
 LAST = GROUPS - 1
 WARM_MATMULS = 3
+LATER_FIRST = (1, 0)
 SQUARED_BY_VECTOR = (1,)
 LOAD_AHEAD = 7
 CAND_BY_PE = range(4, GROUPS)
@@ -194,8 +195,8 @@ def tile_liquidmemorycell_pb_t_kernel(
             old_tiles[g] = old
             gap_tiles[g] = gap
 
-        def blend_new(g, pairs=(0, 1)):
-            if pairs[0] == 0:
+        def blend_new(g, pairs=LATER_FIRST):
+            if g not in m_tiles:
                 m_tile = rows_out.tile([P, TILES, FEAT], F32)
                 m_tiles[g] = m_tile
             for pair in pairs:

import math
from contextlib import ExitStack

import concourse.mybir as mybir
from concourse.masks import make_identity

F32 = mybir.dt.float32
BF16 = mybir.dt.bfloat16
I32 = mybir.dt.int32
U32 = mybir.dt.uint32
U8 = mybir.dt.uint8
FP8X4 = mybir.dt.float8_e4m3fn_x4
ACT = mybir.ActivationFunctionType
ALU = mybir.AluOpType

P = 128
ROWS = 8192
FEAT = 256
K = 2 * FEAT
TILES = 4
GROUP_ROWS = TILES * P
GROUPS = ROWS // GROUP_ROWS
PAIRS = TILES // 2
BLOCKS = 4
KEEP_BLOCKS, UPDATE_BLOCKS = (0, 1), (2, 3)
LAST = GROUPS - 1
WARM_MATMULS = 3
LATER_FIRST = (1, 0)
SQUARED_BY_VECTOR = (1,)
LOAD_AHEAD = 7
CAND_BY_PE = range(4, GROUPS)
SCALED_BY_SCALAR = {12: (0, 1)}

FLOPS = 2 * ROWS * K * 2 * FEAT

LEAST_DECAY = 0.1 + 1e-6
SPAN = 10.0 - 0.1
MOST_DECAY = LEAST_DECAY + SPAN
SHIFT = math.log(MOST_DECAY / LEAST_DECAY)
BETA = SPAN / (LEAST_DECAY * MOST_DECAY)
KEEP_FLOOR = LEAST_DECAY / SPAN
H_SQ_FLOOR = 1e-6 * 1e-6
M_SQ_FLOOR = (1e-12 / BETA) * (1e-12 / BETA)


def live(g):
    return 0 <= g < GROUPS


def tile_liquidmemorycell_pb_t_kernel(
    tc, x, h, h_candidate, Wd_words, Wd_scales, bd, Wu_words, Wu_scales, bu, out
):
    nc = tc.nc
    h_rows = h.rearrange("(g p j) f -> g p j f", p=P, j=TILES)
    x_rows = x.rearrange("(g p j) f -> g p j f", p=P, j=TILES)
    cand_rows = h_candidate.rearrange("(g p j) f -> g p j f", p=P, j=TILES)
    out_rows = out.rearrange("(g p j) f -> g p j f", p=P, j=TILES)

    with ExitStack() as stack:
        const = stack.enter_context(tc.tile_pool(name="const", bufs=1))
        rows_in = stack.enter_context(tc.tile_pool(name="rows_in", bufs=LOAD_AHEAD + 1))
        quant = stack.enter_context(tc.tile_pool(name="quant", bufs=4))
        gates_sb = stack.enter_context(tc.tile_pool(name="gates_sb", bufs=3))
        work = stack.enter_context(tc.tile_pool(name="work", bufs=2 * PAIRS))
        rows_out = stack.enter_context(tc.tile_pool(name="rows_out", bufs=5))
        stats = stack.enter_context(tc.tile_pool(name="stats", bufs=8))
        ct_ps = stack.enter_context(tc.psum_pool(name="ct_ps", bufs=2))
        sum_ps = stack.enter_context(tc.psum_pool(name="sum_ps", bufs=2))
        back_ps = stack.enter_context(tc.psum_pool(name="back_ps", bufs=3))
        cand_ps = stack.enter_context(tc.psum_pool(name="cand_ps", bufs=1))
        stack.enter_context(tc.manual_schedule())

        c_tiles, cand_tiles, cand_banks, plane_sets, grouped_tiles, code_tiles, plane_tiles = {}, {}, {}, {}, {}, {}, {}
        sum_tiles, gate_tiles, keep_banks, update_banks = {}, {}, {}, {}
        old_tiles, gap_tiles, m_tiles, h_sq_tiles, m_sq_tiles, h_inv_tiles, ratio_tiles, root_tiles = {}, {}, {}, {}, {}, {}, {}, {}
        h_floored_tiles, result_tiles = {}, {}

        def load_c(g, tiles_at_once=TILES):
            c_tile = rows_in.tile([P, TILES, K], BF16)
            for first in range(0, TILES, tiles_at_once):
                tiles = slice(first, first + tiles_at_once)
                nc.sync.dma_start(out=c_tile[:, tiles, 0:FEAT], in_=h_rows[g][:, tiles, :])
                nc.sync.dma_start(out=c_tile[:, tiles, FEAT:K], in_=x_rows[g][:, tiles, :])
            c_tiles[g] = c_tile

        def load_cand(g):
            cand = rows_in.tile([P, TILES, FEAT], BF16)
            nc.sync.dma_start(out=cand[:], in_=cand_rows[g])
            cand_tiles[g] = cand

        def load_weight(first, words, scales):
            cols = slice(first, first + FEAT)
            nc.sync.dma_start(
                out=w_words[:, cols].bitcast(I32), in_=words.rearrange("g p n t -> (g p) (n t)").bitcast(I32)
            )
            for quadrant in range(4):
                nc.sync.dma_start(
                    out=w_plane[32 * quadrant : 32 * quadrant + 4, cols].bitcast(I32),
                    in_=scales[0, 4 * quadrant : 4 * quadrant + 4, :].bitcast(I32),
                )

        def turn_c(g, pairs=(0, 1)):
            c_words = c_tiles[g][:].rearrange("p j k -> p (j k)").bitcast(F32)
            words_in_row = K // 2
            for pair in pairs:
                planes = ct_ps.tile([P, 2, 2, P], F32)
                for jj in range(2):
                    first = (2 * pair + jj) * words_in_row
                    for u in range(2):
                        nc.tensor.transpose(
                            planes[:, jj, u, :], c_words[:, first + u : first + words_in_row : 2], identity[:]
                        )
                plane_sets[g, pair] = planes

        def lay_out_c(g):
            grouped = quant.tile([P, GROUP_ROWS * 4], BF16, align_bytes=64)
            grouped_words = grouped[:].bitcast(F32).rearrange("p (j b u) -> p j b u", j=TILES, u=2)
            nc.scalar.copy(out=grouped_words[:, 0:2], in_=plane_sets[g, 0][:].rearrange("p j u b -> p j b u"))
            nc.vector.tensor_copy(out=grouped_words[:, 2:4], in_=plane_sets[g, 1][:].rearrange("p j u b -> p j b u"))
            grouped_tiles[g] = grouped

        def quantise_c(g):
            codes = quant.tile([P, GROUP_ROWS], U32, align_bytes=64)
            plane = quant.tile([P, GROUP_ROWS], U8, align_bytes=64)
            nc.vector.quantize_mx(out=codes[:].bitcast(FP8X4), scales=plane[:], in_=grouped_tiles[g][:])
            code_tiles[g] = codes
            plane_tiles[g] = plane

        def multiply(g, blocks):
            for blk in blocks:
                acc = sum_ps.tile([P, GROUP_ROWS], F32)
                cols = slice(blk * P, (blk + 1) * P)
                nc.tensor.matmul_mx(
                    out=acc[:],
                    lhsT=w_words[:, cols].bitcast(FP8X4),
                    lhsT_scale=w_plane[:, cols],
                    rhs=code_tiles[g][:].bitcast(FP8X4),
                    rhs_scale=plane_tiles[g][:],
                    start=True,
                    stop=True,
                )
                sum_tiles[g, blk] = acc

        def sigmoids(g, blocks):
            if g not in gate_tiles:
                gate_T = gates_sb.tile([P, BLOCKS, GROUP_ROWS], F32)
                gate_tiles[g] = gate_T
            for blk in blocks:
                nc.scalar.activation(
                    out=gate_tiles[g][:, blk, :],
                    in_=sum_tiles[g, blk][:],
                    func=ACT.Sigmoid,
                    bias=bias_cols[:, blk : blk + 1],
                    scale=(-1.0 if blk in KEEP_BLOCKS else 1.0),
                )

        def bring_back(g, blocks, banks):
            for pair in range(PAIRS):
                bank = back_ps.tile([P, 2, FEAT], F32)
                for jj in range(2):
                    rows = slice((2 * pair + jj) * P, (2 * pair + jj + 1) * P)
                    for half, blk in enumerate(blocks):
                        nc.tensor.transpose(
                            bank[:, jj, half * P : (half + 1) * P], gate_tiles[g][:, blk, rows], identity[:]
                        )
                banks[g, pair] = bank

        def copy_cand(g, pair):
            if g not in CAND_BY_PE:
                cand_banks[g] = cand_tiles[g]
                return
            if pair == 0:
                bank = cand_ps.tile([P, TILES, FEAT], BF16)
                cand_banks[g] = bank
            tiles = slice(2 * pair, 2 * pair + 2)
            nc.tensor.matmul(
                cand_banks[g][:, tiles, :], lhsT=identity_bf16[:], rhs=cand_tiles[g][:, tiles, :], start=True, stop=True
            )

        def blend_old(g):
            old = work.tile([P, TILES, FEAT], F32)
            for pair in range(PAIRS):
                tiles = slice(2 * pair, 2 * pair + 2)
                nc.vector.scalar_tensor_tensor(
                    out=old[:, tiles, :], in0=keep_banks[g, pair][:], scalar=KEEP_FLOOR,
                    in1=c_tiles[g][:, tiles, 0:FEAT], op0=ALU.add, op1=ALU.mult,
                )
            gap = work.tile([P, TILES, FEAT], F32)
            for pair in range(PAIRS):
                tiles = slice(2 * pair, 2 * pair + 2)
                nc.vector.scalar_tensor_tensor(
                    out=gap[:, tiles, :], in0=cand_banks[g][:, tiles, :], scalar=1.0 / BETA, in1=old[:, tiles, :],
                    op0=ALU.mult, op1=ALU.subtract,
                )
            old_tiles[g] = old
            gap_tiles[g] = gap

        def blend_new(g, pairs=LATER_FIRST):
            if g not in m_tiles:
                m_tile = rows_out.tile([P, TILES, FEAT], F32)
                m_tiles[g] = m_tile
            for pair in pairs:
                tiles = slice(2 * pair, 2 * pair + 2)
                step = work.tile([P, 2, FEAT], F32)
                nc.vector.tensor_tensor(
                    out=step[:], in0=update_banks[g, pair][:], in1=gap_tiles[g][:, tiles, :], op=ALU.mult
                )
                adder = nc.vector if g == LAST else nc.gpsimd
                adder.tensor_tensor(
                    out=m_tiles[g][:, tiles, :], in0=step[:], in1=old_tiles[g][:, tiles, :], op=ALU.add
                )

        def square_h(g):
            if g % 2 == 0:
                sq = stats.tile([P, 2, TILES], F32, name="h_sq")
                h_sq_tiles[g] = sq
                h_sq_tiles[g + 1] = sq
            unread = work.tile([P, TILES, FEAT], BF16, name="unread")
            for j in range(TILES):
                h_row = c_tiles[g][:, j, 0:FEAT]
                if g in SQUARED_BY_VECTOR:
                    nc.vector.scalar_tensor_tensor(
                        out=unread[:, j, :], in0=h_row, scalar=1.0, in1=h_row, op0=ALU.mult, op1=ALU.mult,
                        accum_out=h_sq_tiles[g][:, g % 2, j : j + 1],
                    )
                else:
                    nc.scalar.activation(
                        out=unread[:, j, :], in_=h_row, func=ACT.Square,
                        accum_out=h_sq_tiles[g][:, g % 2, j : j + 1],
                    )

        def square_m(g, pair):
            if pair == 0:
                sq = stats.tile([P, TILES], F32, name="m_sq")
                m_sq_tiles[g] = sq
            unread = work.tile([P, 2, FEAT], BF16, name="unread_m")
            for jj in range(2):
                j = 2 * pair + jj
                nc.scalar.activation(
                    out=unread[:, jj, :], in_=m_tiles[g][:, j, :], func=ACT.Square,
                    accum_out=m_sq_tiles[g][:, j : j + 1],
                )

        def floor_h(g):
            floored = stats.tile([P, 2, TILES], F32, name="h_floored")
            nc.vector.tensor_scalar(out=floored[:], in0=h_sq_tiles[g][:], scalar1=H_SQ_FLOOR, scalar2=None, op0=ALU.max)
            h_floored_tiles[g] = floored

        def invert_h(g):
            inv = stats.tile([P, 2, TILES], F32, name="h_inv")
            nc.vector.reciprocal(out=inv[:], in_=h_floored_tiles[g][:])
            h_inv_tiles[g] = inv[:, 0, :]
            h_inv_tiles[g + 1] = inv[:, 1, :]

        def ratio(g, cols=slice(0, TILES)):
            if cols.start == 0:
                quotient = stats.tile([P, TILES], F32, name="quotient")
                ratio_tiles[g] = quotient
            nc.vector.scalar_tensor_tensor(
                out=ratio_tiles[g][:, cols], in0=m_sq_tiles[g][:, cols], scalar=M_SQ_FLOOR,
                in1=h_inv_tiles[g][:, cols], op0=ALU.max, op1=ALU.mult,
            )

        def inverse_root(g, cols=slice(0, TILES)):
            if cols.start == 0:
                root = stats.tile([P, TILES], F32, name="root")
                root_tiles[g] = root
            nc.gpsimd.tensor_tensor(
                out=root_tiles[g][:, cols], in0=ratio_tiles[g][:, cols], in1=minus_half[:, cols], op=ALU.pow
            )

        def finish(g, tiles=slice(0, TILES)):
            if tiles.start == 0:
                result = rows_out.tile([P, TILES, FEAT], F32)
                result_tiles[g] = result
            result = result_tiles[g]
            for j in range(tiles.start, tiles.stop):
                if j in SCALED_BY_SCALAR.get(g, ()):
                    nc.scalar.activation(
                        out=result[:, j, :], in_=m_tiles[g][:, j, :], func=ACT.Copy, scale=root_tiles[g][:, j : j + 1]
                    )
                else:
                    nc.vector.tensor_scalar(
                        out=result[:, j, :], in0=m_tiles[g][:, j, :], scalar1=root_tiles[g][:, j : j + 1],
                        scalar2=None, op0=ALU.mult,
                    )
            nc.sync.dma_start(out=out_rows[g][:, tiles, :], in_=result[:, tiles, :])

        load_c(0, tiles_at_once=2)

        warm = const.tile([P, 1], F32)
        nc.vector.memset(warm[:], 0.0)
        nc.scalar.activation(out=warm[:], in_=warm[:], func=ACT.Sigmoid)

        identity = const.tile([P, P], F32)
        make_identity(nc, identity[:])
        minus_half = const.tile([P, TILES], F32)
        nc.gpsimd.memset(minus_half[:], -0.5)
        w_words = const.tile([P, 2 * FEAT], U32, align_bytes=64)
        w_plane = const.tile([P, 2 * FEAT], U8, align_bytes=64)
        bias_rows = const.tile([P, P], BF16)
        nc.vector.memset(bias_rows[:], 0.0)
        nc.vector.memset(w_plane[:].bitcast(I32), 0)
        nc.sync.dma_start(out=bias_rows[0:2, :], in_=bd.rearrange("(r c) -> r c", c=P))
        nc.sync.dma_start(out=bias_rows[2:4, :], in_=bu.rearrange("(r c) -> r c", c=P))
        load_weight(0, Wd_words, Wd_scales)
        load_c(1)
        load_weight(FEAT, Wu_words, Wu_scales)
        load_c(2)
        load_cand(0)
        load_c(3)
        for g in range(4, LOAD_AHEAD):
            load_cand(g - 3)
            load_c(g)

        identity_bf16 = const.tile([P, P], BF16)
        nc.vector.tensor_copy(out=identity_bf16[:], in_=identity[:])
        bias_cols = const.tile([P, BLOCKS], F32)

        warm_ps = back_ps.tile([P, 2, FEAT], F32, name="bank")

        def warm_up(part):
            nc.tensor.matmul(
                warm_ps[:, part // 2 % 2, part % 2 * P : (part % 2 + 1) * P], lhsT=identity[:], rhs=identity[:],
                start=True, stop=True,
            )

        for part in range(WARM_MATMULS):
            warm_up(part)

        turn_c(0)
        for part in range(WARM_MATMULS):
            warm_up(part)
        lay_out_c(0)
        bias_ps = ct_ps.tile([P, P], BF16, name="planes")
        nc.tensor.transpose(bias_ps[:], bias_rows[:], identity_bf16[:])
        quantise_c(0)
        nc.vector.tensor_scalar(
            out=bias_cols[:, 0:2], in0=bias_ps[:, 0:2], scalar1=-1.0, scalar2=-SHIFT, op0=ALU.mult, op1=ALU.add
        )
        nc.vector.tensor_copy(out=bias_cols[:, 2:4], in_=bias_ps[:, 2:4])
        square_h(0)
        square_h(1)
        multiply(0, KEEP_BLOCKS)
        turn_c(1)
        sigmoids(0, KEEP_BLOCKS)
        multiply(0, UPDATE_BLOCKS)
        lay_out_c(1)
        bring_back(0, KEEP_BLOCKS, keep_banks)
        sigmoids(0, UPDATE_BLOCKS)
        quantise_c(1)
        turn_c(2)
        multiply(1, KEEP_BLOCKS)
        bring_back(0, UPDATE_BLOCKS, update_banks)
        copy_cand(0, 0)
        blend_old(0)
        lay_out_c(2)
        quantise_c(2)
        copy_cand(1, 0)

        for t in range(LAST):
            if live(t + LOAD_AHEAD):
                load_c(t + LOAD_AHEAD)
            if live(t + LOAD_AHEAD - 3):
                load_cand(t + LOAD_AHEAD - 3)
            blend_new(t)
            if live(t - 2):
                inverse_root(t - 2)
            if t < LAST - 1:
                sigmoids(t + 1, KEEP_BLOCKS)
                multiply(t + 1, UPDATE_BLOCKS)
            if t == 0:
                turn_c(3)
            bring_back(t + 1, KEEP_BLOCKS, keep_banks)
            if 0 < t and live(t + 3):
                lay_out_c(t + 3)
            if t < LAST - 1:
                sigmoids(t + 1, UPDATE_BLOCKS)
            if t == 0:
                lay_out_c(3)
            if t < LAST - 2:
                multiply(t + 2, (0,))
            copy_cand(t + 1, 1)
            if live(t + 4):
                turn_c(t + 4)
            blend_old(t + 1)
            if t < LAST - 2:
                multiply(t + 2, (1,))
            bring_back(t + 1, UPDATE_BLOCKS, update_banks)
            if live(t - 1):
                square_m(t - 1, 0)
                square_m(t - 1, 1)
            if t == LAST - 2:
                multiply(LAST, KEEP_BLOCKS)
                sigmoids(LAST, KEEP_BLOCKS)
                multiply(LAST, UPDATE_BLOCKS)
                sigmoids(LAST, UPDATE_BLOCKS)
            if live(t + 2):
                copy_cand(t + 2, 0)
            if live(t + 2):
                square_h(t + 2)
            if live(t + 3):
                quantise_c(t + 3)
            if t % 2 == 0:
                floor_h(t)
            if live(t - 3):
                finish(t - 3)
            if t % 2 == 0:
                invert_h(t)
            if live(t - 1):
                ratio(t - 1)

        first_pair, second_pair = slice(0, 2), slice(2, TILES)
        blend_new(LAST, (0,))
        inverse_root(LAST - 2)
        square_m(LAST - 1, 0)
        square_m(LAST - 1, 1)
        ratio(LAST - 1)
        inverse_root(LAST - 1)
        finish(LAST - 3)
        blend_new(LAST, (1,))
        square_m(LAST, 0)
        ratio(LAST, first_pair)
        inverse_root(LAST, first_pair)
        square_m(LAST, 1)
        finish(LAST - 2)
        ratio(LAST, second_pair)
        inverse_root(LAST, second_pair)
        finish(LAST - 1)
        finish(LAST, first_pair)
        finish(LAST, second_pair)
